import numpy as np
import ml_dtypes


def mxq(x, axis, fmt="e4m3"):
    dtype, down = {"e4m3": (ml_dtypes.float8_e4m3fn, 7), "e5m2": (ml_dtypes.float8_e5m2, 14)}[fmt]
    v = np.moveaxis(np.asarray(x, np.float32).astype(ml_dtypes.bfloat16).astype(np.float64), axis, -1)
    blocks = v.reshape(v.shape[:-1] + (-1, 32))
    amax = np.abs(blocks).max(-1, keepdims=True)
    byte = np.maximum(np.where(amax > 0, np.frexp(amax)[1] - 1 + 127, 0) - down, 1)
    scale = np.exp2(byte - 127.0)
    codes = (blocks / scale).astype(np.float32).astype(dtype).astype(np.float64)
    return np.moveaxis((codes * scale).reshape(v.shape), -1, axis)


WIDE = False


def mx_kscale(k):
    if not WIDE:
        return np.ones(k)
    levels = np.array([10, -10, 5, -5, 0])
    a = np.random.permutation(np.resize(levels, k // 512 * 4)).reshape(k // 512, 4)
    idx = np.arange(k)
    return np.exp2(a[idx // 512, idx % 128 // 32])


BF16 = ml_dtypes.bfloat16


def bf(x):
    return np.asarray(x, np.float32).astype(BF16)


def f64(x):
    return np.asarray(x).astype(np.float64)


B, DD, DK, CI, CO, L, NLC, PAD, KL = 1, 2, 2, 512, 128, 256, 4, 4, 9


def seg_lengths():
    cover = (L + PAD + PAD) // NLC - PAD - PAD
    lens = [cover] * NLC
    lens[-1] = L - cover * (NLC - 1)
    return lens


def setup_inputs():
    s = mx_kscale(CI)
    x = np.random.standard_normal((B, DD, DK, CI, L)) * s[:, None]
    weight = np.random.standard_normal((DD, DK, CO, CI, NLC, KL)) / np.sqrt(CI * KL) / s[:, None, None]
    bias = np.random.standard_normal((DD, DK, CO, NLC)) * 0.5
    return {"x": bf(x), "weight": bf(weight[..., None, :]), "conv_bias_param": bf(bias[..., None])}


def reference(x, weight, conv_bias_param):
    xq = mxq(f64(x), 3, "e4m3")
    wq = mxq(f64(weight), 3, "e4m3")
    bias = f64(conv_bias_param)
    outs, start = [], 0
    for i, ln in enumerate(seg_lengths()):
        acc = np.zeros((B, DD, DK, CO, ln))
        for f in range(KL):
            lo = max(start, PAD - f)
            hi = min(start + ln, L + PAD - f)
            xs = xq[..., lo + f - PAD:hi + f - PAD].swapaxes(-1, -2)
            wf = wq[:, :, :, :, i, 0, f].swapaxes(-1, -2)
            acc[..., lo - start:hi - start] += (xs @ wf).swapaxes(-1, -2)
        outs.append(acc + bias[None, :, :, :, i, :])
        start += ln
    return np.concatenate(outs, axis=-1)

@@ -1,0 +1,127 @@
+from contextlib import ExitStack
+
+import concourse.mybir as mybir
+
+FP8X4 = mybir.dt.float8_e4m3fn_x4
+BF16 = mybir.dt.bfloat16
+F32 = mybir.dt.float32
+U32 = mybir.dt.uint32
+U8 = mybir.dt.uint8
+
+P = 128
+GROUPS = 4
+CO = 128
+CI = 512
+PACK = 4
+L = 256
+NSEG = 4
+TAPS = 9
+SF = NSEG * TAPS
+R = 4
+A = L // R
+EXT = R + TAPS - 1
+XCOLS = EXT * A
+NO = 32
+VG = 7
+
+FLOPS = 2 * GROUPS * CO * CI * TAPS * L
+
+
+def tile_partiallyunsharedconv1d_pa_kernel(tc, x, weight, conv_bias_param, out):
+    nc = tc.nc
+    xv = x.rearrange("b d k (p j) l -> (b d k) p j l", j=PACK)
+    wv = weight.rearrange("d k o (p j) s u f -> (d k) p o (j s u f)", j=PACK)
+    bv = conv_bias_param.rearrange("d k o s u -> o (d k) (s u)")
+    ov = out.rearrange("b d k o l -> (b d k) o l")
+
+    with ExitStack() as ctx:
+        keep = ctx.enter_context(tc.tile_pool(name="keep", bufs=1))
+        rawp = ctx.enter_context(tc.tile_pool(name="rawp", bufs=6))
+        grpp = ctx.enter_context(tc.tile_pool(name="grpp", bufs=2))
+        codp = ctx.enter_context(tc.tile_pool(name="codp", bufs=2))
+        outp = ctx.enter_context(tc.tile_pool(name="outp", bufs=2))
+        psum = ctx.enter_context(tc.psum_pool(name="psum", bufs=4))
+
+        xg = keep.tile([P, GROUPS, EXT, A, PACK], BF16, align_bytes=64)
+        nc.vector.memset(xg[:, :, 0:R, 0:1, :], 0.0)
+        nc.vector.memset(xg[:, :, 2 * R : EXT, A - 1 : A, :], 0.0)
+        xraw = keep.tile([P, GROUPS, PACK, L], BF16)
+        bias_bf = keep.tile([P, GROUPS * NSEG], BF16)
+        for g in range(GROUPS):
+            nc.scalar.dma_start(out=xraw[:, g], in_=xv[g])
+        nc.scalar.dma_start(out=bias_bf[:].rearrange("o (g s) -> o g s", s=NSEG), in_=bv)
+        bias_f = keep.tile([P, GROUPS * NSEG], F32)
+        nc.vector.tensor_copy(out=bias_f[:], in_=bias_bf[:])
+        xc = keep.tile([P, GROUPS * XCOLS], U32, align_bytes=64)
+        xs = keep.tile([P, GROUPS * XCOLS], U8, align_bytes=64)
+        for g in range(GROUPS):
+            src = xraw[:, g].rearrange("p j (a r) -> p r a j", r=R)
+            if g < 2:
+                nc.vector.tensor_copy(out=xg[:, g, R : 2 * R], in_=src)
+            else:
+                nc.scalar.copy(out=xg[:, g, R : 2 * R], in_=src)
+        mid = xg[:, :, R : 2 * R].rearrange("p g r a j -> p g r (a j)")
+        low = xg[:, :, 0:R].rearrange("p g r a j -> p g r (a j)")
+        high = xg[:, :, 2 * R : EXT].rearrange("p g r a j -> p g r (a j)")
+        nc.vector.tensor_copy(out=low[:, :, :, PACK:], in_=mid[:, :, :, : (A - 1) * PACK])
+        nc.vector.tensor_copy(out=high[:, :, :, : (A - 1) * PACK], in_=mid[:, :, :, PACK:])
+        xflat = xg[:].rearrange("p g r a j -> p (g r a j)")
+        for c in range(3):
+            nc.vector.quantize_mx(
+                out=xc[:, c * 1024 : (c + 1) * 1024].bitcast(FP8X4),
+                scales=xs[:, c * 1024 : (c + 1) * 1024],
+                in_=xflat[:, c * 4096 : (c + 1) * 4096],
+            )
+
+        for g in range(GROUPS):
+            grp = grpp.tile([P, SF, CO * PACK], BF16, align_bytes=64)
+            for o0 in range(0, CO, NO):
+                raw = rawp.tile([P, NO * PACK * SF], BF16)
+                nc.sync.dma_start(
+                    out=raw[:].rearrange("p (o e) -> p o e", o=NO),
+                    in_=wv[g][:, o0 : o0 + NO, :],
+                )
+                src = raw[:].rearrange("p (m a q) -> p a m q", a=TAPS, q=4)
+                dst = grp[:, :, PACK * o0 : PACK * (o0 + NO)].rearrange("p (a q) m -> p a m q", q=4)
+                nc.vector.tensor_copy(out=dst[:, 0:VG], in_=src[:, 0:VG])
+                nc.scalar.copy(out=dst[:, VG:TAPS], in_=src[:, VG:TAPS])
+
+            wc = codp.tile([P, SF * CO], U32, align_bytes=64)
+            ws = codp.tile([P, SF * CO], U8, align_bytes=64)
+            for s0, n in ((0, 8), (8, 8), (16, 8), (24, 8), (32, 4)):
+                nc.vector.quantize_mx(
+                    out=wc[:, s0 * CO : (s0 + n) * CO].bitcast(FP8X4),
+                    scales=ws[:, s0 * CO : (s0 + n) * CO],
+                    in_=grp[:, s0 : s0 + n, :].rearrange("p s m -> p (s m)"),
+                )
+
+            accs = []
+            for s in range(NSEG):
+                if s % 2 == 0:
+                    bank = psum.tile([P, 2 * L], F32)
+                acc = bank[:, (s % 2) * L : (s % 2 + 1) * L]
+                accs.append(acc.rearrange("p (r a) -> p a r", r=R))
+                for f in range(TAPS):
+                    w0 = (s * TAPS + f) * CO
+                    x0 = g * XCOLS + A * f
+                    nc.tensor.matmul_mx(
+                        out=acc,
+                        lhsT=wc[:, w0 : w0 + CO].bitcast(FP8X4),
+                        lhsT_scale=ws[:, w0 : w0 + CO],
+                        rhs=xc[:, x0 : x0 + L].bitcast(FP8X4),
+                        rhs_scale=xs[:, x0 : x0 + L],
+                        start=(f == 0),
+                        stop=(f == TAPS - 1),
+                    )
+            osb = outp.tile([P, L], F32)
+            oar = osb[:].rearrange("p (a r) -> p a r", r=R)
+            for s, a0, a1, r0 in ((0, 0, 15, 0), (1, 15, 29, 0), (1, 14, 15, 2), (2, 29, 44, 0), (3, 44, 64, 0), (3, 43, 44, 2)):
+                nc.vector.tensor_scalar_add(
+                    out=oar[:, a0:a1, r0:R],
+                    in0=accs[s][:, a0:a1, r0:R],
+                    scalar1=bias_f[:, g * NSEG + s : g * NSEG + s + 1],
+                )
+            if g < GROUPS - 1:
+                nc.gpsimd.dma_start(out=ov[g], in_=osb[:])
+            else:
+                nc.sync.dma_start(out=ov[g], in_=osb[:])

@@ -1,6 +1,7 @@
 from contextlib import ExitStack
 
 import concourse.mybir as mybir
+from concourse.masks import make_identity
 
 FP8X4 = mybir.dt.float8_e4m3fn_x4
 BF16 = mybir.dt.bfloat16
@@ -21,37 +22,90 @@ R = 4
 A = L // R
 EXT = R + TAPS - 1
 XCOLS = EXT * A
-NO = 32
-VG = 7
+HALF = CI // 2
+QUADS = SF // 4
+PIECES = 4
+STEPS = GROUPS * QUADS
+LEAD = 2
+BURST = 3
+
+S_UNITS = (3, 7, 12, 16)
+PRE_VQ = 5
+V_EVAC_LAST = (1, 3, 5, 7)
+
+CUTS = ((0, 0, 15, 0), (1, 15, 29, 0), (1, 14, 15, 2), (2, 29, 44, 0), (3, 44, 64, 0), (3, 43, 44, 2))
 
 FLOPS = 2 * GROUPS * CO * CI * TAPS * L
 
 
 def tile_partiallyunsharedconv1d_pa_kernel(tc, x, weight, conv_bias_param, out):
     nc = tc.nc
-    xv = x.rearrange("b d k (p j) l -> (b d k) p j l", j=PACK)
-    wv = weight.rearrange("d k o (p j) s u f -> (d k) p o (j s u f)", j=PACK)
+    xv = x.rearrange("b d k (h p e) l -> (b d k) p h (e l)", h=2, e=2)
+    wv = weight.rearrange("d k o i s u f -> (d k) o (i s u f)")
     bv = conv_bias_param.rearrange("d k o s u -> o (d k) (s u)")
     ov = out.rearrange("b d k o l -> (b d k) o l")
+    CH = HALF * SF
 
     with ExitStack() as ctx:
+        ctx.enter_context(tc.manual_schedule())
         keep = ctx.enter_context(tc.tile_pool(name="keep", bufs=1))
-        rawp = ctx.enter_context(tc.tile_pool(name="rawp", bufs=6))
-        grpp = ctx.enter_context(tc.tile_pool(name="grpp", bufs=2))
-        codp = ctx.enter_context(tc.tile_pool(name="codp", bufs=2))
+        rawp = ctx.enter_context(tc.tile_pool(name="rawp", bufs=3))
+        w2p = ctx.enter_context(tc.tile_pool(name="w2p", bufs=4))
+        grpp = ctx.enter_context(tc.tile_pool(name="grpp", bufs=4))
+        codp = ctx.enter_context(tc.tile_pool(name="codp", bufs=4))
         outp = ctx.enter_context(tc.tile_pool(name="outp", bufs=2))
-        psum = ctx.enter_context(tc.psum_pool(name="psum", bufs=4))
+        ptp = ctx.enter_context(tc.psum_pool(name="ptp", bufs=6))
+        accp = ctx.enter_context(tc.psum_pool(name="accp", bufs=2))
+
+        ident = keep.tile([P, P], F32)
+        make_identity(nc, ident[:])
+        bias_bf = keep.tile([P, GROUPS * NSEG], BF16)
+        nc.gpsimd.dma_start(out=bias_bf[:].rearrange("o (g s) -> o g s", s=NSEG), in_=bv)
+
+        raws = {}
+        w2s = {}
+
+        def load(c, pieces):
+            raw = rawp.tile([P, CH], BF16, name="raw")
+            raws[c] = raw
+            g, h = divmod(c, 2)
+            w = CH // pieces
+            for i in range(pieces):
+                nc.sync.dma_start(
+                    out=raw[:, i * w : (i + 1) * w],
+                    in_=wv[g][:, h * CH + i * w : h * CH + (i + 1) * w],
+                )
+
+        def regroup(eng_is_vector, c, q0, q1, m0, m1):
+            if c not in w2s:
+                w2 = w2p.tile([P, SF, HALF], BF16, name="w2")
+                w2s[c] = w2
+            src = raws[c][:, m0 * SF : m1 * SF].rearrange("p (m a q) -> p a m q", a=QUADS, q=4)
+            dst = w2s[c][:, :, m0:m1].rearrange("p (a q) m -> p a m q", q=4)
+            if eng_is_vector:
+                nc.vector.tensor_copy(out=dst[:, q0:q1], in_=src[:, q0:q1])
+            else:
+                nc.scalar.copy(out=dst[:, q0:q1], in_=src[:, q0:q1])
+
+        xraw = keep.tile([P, GROUPS, PACK, L], BF16)
+        for g in range(GROUPS):
+            nc.sync.dma_start(out=xraw[:, g].rearrange("p (h e) l -> p h (e l)", h=2), in_=xv[g])
+        load(0, PIECES)
+        load(1, PIECES)
+        load(2, 1)
+
+        mp = HALF // PIECES
+
+        def first_pieces(on_vector, k):
+            c, i = divmod(k, PIECES)
+            if on_vector:
+                regroup(True, c, 0, PRE_VQ, i * mp, (i + 1) * mp)
+            else:
+                regroup(False, c, PRE_VQ, QUADS, i * mp, (i + 1) * mp)
 
         xg = keep.tile([P, GROUPS, EXT, A, PACK], BF16, align_bytes=64)
         nc.vector.memset(xg[:, :, 0:R, 0:1, :], 0.0)
         nc.vector.memset(xg[:, :, 2 * R : EXT, A - 1 : A, :], 0.0)
-        xraw = keep.tile([P, GROUPS, PACK, L], BF16)
-        bias_bf = keep.tile([P, GROUPS * NSEG], BF16)
-        for g in range(GROUPS):
-            nc.scalar.dma_start(out=xraw[:, g], in_=xv[g])
-        nc.scalar.dma_start(out=bias_bf[:].rearrange("o (g s) -> o g s", s=NSEG), in_=bv)
-        bias_f = keep.tile([P, GROUPS * NSEG], F32)
-        nc.vector.tensor_copy(out=bias_f[:], in_=bias_bf[:])
         xc = keep.tile([P, GROUPS * XCOLS], U32, align_bytes=64)
         xs = keep.tile([P, GROUPS * XCOLS], U8, align_bytes=64)
         for g in range(GROUPS):
@@ -60,11 +114,15 @@ def tile_partiallyunsharedconv1d_pa_kernel(tc, x, weight, conv_bias_param, out):
                 nc.vector.tensor_copy(out=xg[:, g, R : 2 * R], in_=src)
             else:
                 nc.scalar.copy(out=xg[:, g, R : 2 * R], in_=src)
+        for k in range(2 * PIECES):
+            first_pieces(False, k)
+        first_pieces(True, 0)
         mid = xg[:, :, R : 2 * R].rearrange("p g r a j -> p g r (a j)")
         low = xg[:, :, 0:R].rearrange("p g r a j -> p g r (a j)")
         high = xg[:, :, 2 * R : EXT].rearrange("p g r a j -> p g r (a j)")
         nc.vector.tensor_copy(out=low[:, :, :, PACK:], in_=mid[:, :, :, : (A - 1) * PACK])
         nc.vector.tensor_copy(out=high[:, :, :, : (A - 1) * PACK], in_=mid[:, :, :, PACK:])
+        first_pieces(True, 1)
         xflat = xg[:].rearrange("p g r a j -> p (g r a j)")
         for c in range(3):
             nc.vector.quantize_mx(
@@ -72,56 +130,120 @@ def tile_partiallyunsharedconv1d_pa_kernel(tc, x, weight, conv_bias_param, out):
                 scales=xs[:, c * 1024 : (c + 1) * 1024],
                 in_=xflat[:, c * 4096 : (c + 1) * 4096],
             )
+            first_pieces(True, 2 + c)
+        bias_f = keep.tile([P, GROUPS * NSEG], F32)
+        nc.vector.tensor_copy(out=bias_f[:], in_=bias_bf[:])
+        for k in range(5, 2 * PIECES):
+            first_pieces(True, k)
+        load(3, 1)
+        load(4, 1)
 
-        for g in range(GROUPS):
-            grp = grpp.tile([P, SF, CO * PACK], BF16, align_bytes=64)
-            for o0 in range(0, CO, NO):
-                raw = rawp.tile([P, NO * PACK * SF], BF16)
-                nc.sync.dma_start(
-                    out=raw[:].rearrange("p (o e) -> p o e", o=NO),
-                    in_=wv[g][:, o0 : o0 + NO, :],
+        pts = {}
+        grps = {}
+        cods = {}
+        accs = {}
+
+        def transposes(n):
+            g, a = divmod(n, QUADS)
+            for b in range(2):
+                pt = ptp.tile([P, 2, 2, CO], F32, name="pt")
+                pts[(n, b)] = pt
+                for s in range(2):
+                    sf = 4 * a + 2 * b + s
+                    for h in range(2):
+                        nc.tensor.transpose(pt[:, s, h, :], w2s[2 * g + h][:, sf, :].bitcast(F32), ident[:])
+
+        def evacuate(n, b, on_vector):
+            if b == 0:
+                grp = grpp.tile([P, 4 * CO * PACK], BF16, name="grp", align_bytes=64)
+                grps[n] = grp
+            half = CO * PACK
+            dst = grps[n][:].bitcast(F32)[:, b * half : (b + 1) * half].rearrange("p (s o h) -> p s o h", s=2, h=2)
+            src = pts[(n, b)][:].rearrange("p s h o -> p s o h")
+            if on_vector:
+                nc.vector.tensor_copy(out=dst, in_=src)
+            else:
+                nc.scalar.copy(out=dst, in_=src)
+
+        def quantise(n):
+            t, j = divmod(n, BURST)
+            if j == 0:
+                wc = codp.tile([P, BURST * 4 * CO], U32, name="wc", align_bytes=64)
+                ws = codp.tile([P, BURST * 4 * CO], U8, name="ws", align_bytes=64)
+                cods[t] = (wc, ws)
+            wc, ws = cods[t]
+            w = 4 * CO
+            nc.vector.quantize_mx(
+                out=wc[:, j * w : (j + 1) * w].bitcast(FP8X4),
+                scales=ws[:, j * w : (j + 1) * w],
+                in_=grps[n][:],
+            )
+
+        def burst(t, j0, j1):
+            g, b = divmod(t, QUADS // BURST)
+            wc, ws = cods[t]
+            for i in range(j0 * 4, j1 * 4):
+                s, f = divmod(b * BURST * 4 + i, TAPS)
+                if f == 0 and s % 2 == 0:
+                    bank = accp.tile([P, 2 * L], F32, name="bank")
+                    accs[(g, s // 2)] = bank
+                acc = accs[(g, s // 2)][:, (s % 2) * L : (s % 2 + 1) * L]
+                x0 = g * XCOLS + A * f
+                nc.tensor.matmul_mx(
+                    out=acc,
+                    lhsT=wc[:, i * CO : (i + 1) * CO].bitcast(FP8X4),
+                    lhsT_scale=ws[:, i * CO : (i + 1) * CO],
+                    rhs=xc[:, x0 : x0 + L].bitcast(FP8X4),
+                    rhs_scale=xs[:, x0 : x0 + L],
+                    start=(f == 0),
+                    stop=(f == TAPS - 1),
                 )
-                src = raw[:].rearrange("p (m a q) -> p a m q", a=TAPS, q=4)
-                dst = grp[:, :, PACK * o0 : PACK * (o0 + NO)].rearrange("p (a q) m -> p a m q", q=4)
-                nc.vector.tensor_copy(out=dst[:, 0:VG], in_=src[:, 0:VG])
-                nc.scalar.copy(out=dst[:, VG:TAPS], in_=src[:, VG:TAPS])
 
-            wc = codp.tile([P, SF * CO], U32, align_bytes=64)
-            ws = codp.tile([P, SF * CO], U8, align_bytes=64)
-            for s0, n in ((0, 8), (8, 8), (16, 8), (24, 8), (32, 4)):
-                nc.vector.quantize_mx(
-                    out=wc[:, s0 * CO : (s0 + n) * CO].bitcast(FP8X4),
-                    scales=ws[:, s0 * CO : (s0 + n) * CO],
-                    in_=grp[:, s0 : s0 + n, :].rearrange("p s m -> p (s m)"),
-                )
+        osbs = {}
 
-            accs = []
-            for s in range(NSEG):
-                if s % 2 == 0:
-                    bank = psum.tile([P, 2 * L], F32)
-                acc = bank[:, (s % 2) * L : (s % 2 + 1) * L]
-                accs.append(acc.rearrange("p (r a) -> p a r", r=R))
-                for f in range(TAPS):
-                    w0 = (s * TAPS + f) * CO
-                    x0 = g * XCOLS + A * f
-                    nc.tensor.matmul_mx(
-                        out=acc,
-                        lhsT=wc[:, w0 : w0 + CO].bitcast(FP8X4),
-                        lhsT_scale=ws[:, w0 : w0 + CO],
-                        rhs=xc[:, x0 : x0 + L].bitcast(FP8X4),
-                        rhs_scale=xs[:, x0 : x0 + L],
-                        start=(f == 0),
-                        stop=(f == TAPS - 1),
-                    )
-            osb = outp.tile([P, L], F32)
-            oar = osb[:].rearrange("p (a r) -> p a r", r=R)
-            for s, a0, a1, r0 in ((0, 0, 15, 0), (1, 15, 29, 0), (1, 14, 15, 2), (2, 29, 44, 0), (3, 44, 64, 0), (3, 43, 44, 2)):
+        def finish(g, part):
+            if part == 0:
+                osb = outp.tile([P, L], F32, name="osb")
+                osbs[g] = osb
+            oar = osbs[g][:].rearrange("p (a r) -> p a r", r=R)
+            for s, a0, a1, r0 in CUTS[3 * part : 3 * part + 3]:
+                acc = accs[(g, s // 2)][:, (s % 2) * L : (s % 2 + 1) * L].rearrange("p (r a) -> p a r", r=R)
                 nc.vector.tensor_scalar_add(
                     out=oar[:, a0:a1, r0:R],
-                    in0=accs[s][:, a0:a1, r0:R],
+                    in0=acc[:, a0:a1, r0:R],
                     scalar1=bias_f[:, g * NSEG + s : g * NSEG + s + 1],
                 )
-            if g < GROUPS - 1:
-                nc.gpsimd.dma_start(out=ov[g], in_=osb[:])
-            else:
-                nc.sync.dma_start(out=ov[g], in_=osb[:])
+            if part == 1:
+                nc.sync.dma_start(out=ov[g], in_=osbs[g][:])
+
+        for n in range(LEAD):
+            transposes(n)
+        for n in range(STEPS + 1):
+            g, a = divmod(n, QUADS)
+            if n + LEAD < STEPS:
+                transposes(n + LEAD)
+            if n < STEPS:
+                last = g == GROUPS - 1
+                evacuate(n, 0, False)
+                if not (last and a in V_EVAC_LAST):
+                    evacuate(n, 1, False)
+                if not last:
+                    for u in (2 * a, 2 * a + 1):
+                        h, q = divmod(u, QUADS)
+                        regroup(u not in S_UNITS, 2 * (g + 1) + h, q, q + 1, 0, HALF)
+                        if q == QUADS - 1 and 2 * (g + 1) + h + 3 < 2 * GROUPS:
+                            load(2 * (g + 1) + h + 3, 1)
+                if last and a in V_EVAC_LAST:
+                    evacuate(n, 1, True)
+            if n > 0:
+                quantise(n - 1)
+                if n > STEPS - BURST:
+                    burst((n - 1) // BURST, (n - 1) % BURST, (n - 1) % BURST + 1)
+                elif n % BURST == 0:
+                    burst(n // BURST - 1, 0, BURST)
+                if n % QUADS == 1 and n > 1:
+                    finish(n // QUADS - 1, 0)
+                    finish(n // QUADS - 1, 1)
+                if n == STEPS - 2:
+                    finish(GROUPS - 1, 0)
+        finish(GROUPS - 1, 1)

@@ -237,13 +237,12 @@ def tile_partiallyunsharedconv1d_pa_kernel(tc, x, weight, conv_bias_param, out):
                     evacuate(n, 1, True)
             if n > 0:
                 quantise(n - 1)
-                if n > STEPS - BURST:
-                    burst((n - 1) // BURST, (n - 1) % BURST, (n - 1) % BURST + 1)
-                elif n % BURST == 0:
-                    burst(n // BURST - 1, 0, BURST)
-                if n % QUADS == 1 and n > 1:
+                if n % QUADS == 2 and n > 2:
                     finish(n // QUADS - 1, 0)
                     finish(n // QUADS - 1, 1)
                 if n == STEPS - 2:
                     finish(GROUPS - 1, 0)
+            if n > 1:
+                burst((n - 2) // BURST, (n - 2) % BURST, (n - 2) % BURST + 1)
+        burst((STEPS - 1) // BURST, (STEPS - 1) % BURST, (STEPS - 1) % BURST + 1)
         finish(GROUPS - 1, 1)

@@ -26,12 +26,17 @@ HALF = CI // 2
 QUADS = SF // 4
 PIECES = 4
 STEPS = GROUPS * QUADS
+TSTEPS = STEPS - QUADS
 LEAD = 2
 BURST = 3
+CH = HALF * SF
+RAWB = 4
+SHIFT = 4
 
 S_UNITS = (3, 7, 12, 16)
+S_TAIL = (1, 2, 4, 5, 7, 8)
 PRE_VQ = 5
-V_EVAC_LAST = (1, 3, 5, 7)
+V_EVAC = (25, 26)
 
 CUTS = ((0, 0, 15, 0), (1, 15, 29, 0), (1, 14, 15, 2), (2, 29, 44, 0), (3, 44, 64, 0), (3, 43, 44, 2))
 
@@ -41,19 +46,21 @@ FLOPS = 2 * GROUPS * CO * CI * TAPS * L
 def tile_partiallyunsharedconv1d_pa_kernel(tc, x, weight, conv_bias_param, out):
     nc = tc.nc
     xv = x.rearrange("b d k (h p e) l -> (b d k) p h (e l)", h=2, e=2)
+    xva = x.rearrange("b d k (p j) l -> (b d k) p (j l)", j=PACK)
     wv = weight.rearrange("d k o i s u f -> (d k) o (i s u f)")
+    wva = weight.rearrange("d k o (p j) s u f -> (d k) p o (j s u f)", j=PACK)
     bv = conv_bias_param.rearrange("d k o s u -> o (d k) (s u)")
     ov = out.rearrange("b d k o l -> (b d k) o l")
-    CH = HALF * SF
+    LASTG = GROUPS - 1
 
     with ExitStack() as ctx:
         ctx.enter_context(tc.manual_schedule())
         keep = ctx.enter_context(tc.tile_pool(name="keep", bufs=1))
-        rawp = ctx.enter_context(tc.tile_pool(name="rawp", bufs=3))
+        rawp = ctx.enter_context(tc.tile_pool(name="rawp", bufs=RAWB))
         w2p = ctx.enter_context(tc.tile_pool(name="w2p", bufs=4))
         grpp = ctx.enter_context(tc.tile_pool(name="grpp", bufs=4))
         codp = ctx.enter_context(tc.tile_pool(name="codp", bufs=4))
-        outp = ctx.enter_context(tc.tile_pool(name="outp", bufs=2))
+        outp = ctx.enter_context(tc.tile_pool(name="outp", bufs=4))
         ptp = ctx.enter_context(tc.psum_pool(name="ptp", bufs=6))
         accp = ctx.enter_context(tc.psum_pool(name="accp", bufs=2))
 
@@ -69,30 +76,67 @@ def tile_partiallyunsharedconv1d_pa_kernel(tc, x, weight, conv_bias_param, out):
             raw = rawp.tile([P, CH], BF16, name="raw")
             raws[c] = raw
             g, h = divmod(c, 2)
-            w = CH // pieces
-            for i in range(pieces):
+            if g == LASTG:
+                half = CO // 2
                 nc.sync.dma_start(
-                    out=raw[:, i * w : (i + 1) * w],
-                    in_=wv[g][:, h * CH + i * w : h * CH + (i + 1) * w],
+                    out=raw[:].rearrange("p (o e) -> p o e", o=half),
+                    in_=wva[g][:, h * half : (h + 1) * half, :],
                 )
+            else:
+                w = CH // pieces
+                for i in range(pieces):
+                    nc.sync.dma_start(
+                        out=raw[:, i * w : (i + 1) * w],
+                        in_=wv[g][:, h * CH + i * w : h * CH + (i + 1) * w],
+                    )
 
-        def regroup(eng_is_vector, c, q0, q1, m0, m1):
+        def copy(on_vector, dst, src):
+            if on_vector:
+                nc.vector.tensor_copy(out=dst, in_=src)
+            else:
+                nc.scalar.copy(out=dst, in_=src)
+
+        def regroup(on_vector, c, q0, q1, m0, m1):
             if c not in w2s:
-                w2 = w2p.tile([P, SF, HALF], BF16, name="w2")
+                w2 = w2p.tile([P, SF, HALF], BF16, name="w2", align_bytes=64)
                 w2s[c] = w2
             src = raws[c][:, m0 * SF : m1 * SF].rearrange("p (m a q) -> p a m q", a=QUADS, q=4)
             dst = w2s[c][:, :, m0:m1].rearrange("p (a q) m -> p a m q", q=4)
-            if eng_is_vector:
-                nc.vector.tensor_copy(out=dst[:, q0:q1], in_=src[:, q0:q1])
-            else:
-                nc.scalar.copy(out=dst[:, q0:q1], in_=src[:, q0:q1])
+            copy(on_vector, dst[:, q0:q1], src[:, q0:q1])
 
-        xraw = keep.tile([P, GROUPS, PACK, L], BF16)
-        for g in range(GROUPS):
-            nc.sync.dma_start(out=xraw[:, g].rearrange("p (h e) l -> p h (e l)", h=2), in_=xv[g])
+        gas = {}
+        ROWS = SF // 2
+
+        def regroup_last(on_vector, h, a):
+            src = raws[2 * LASTG + h][:].rearrange("p (m a q) -> p a m q", a=QUADS, q=4)
+            sf = 4 * a
+            while sf < 4 * a + 4:
+                t, r0 = divmod(sf, ROWS)
+                n = min(4 * a + 4 - sf, ROWS - r0)
+                if t not in gas:
+                    ga = w2p.tile([P, ROWS, CO * PACK], BF16, name="w2", align_bytes=64)
+                    gas[t] = ga
+                dst = gas[t][:, r0 : r0 + n, h * HALF : (h + 1) * HALF].rearrange("p (a q) m -> p a m q", q=n)
+                copy(on_vector, dst, src[:, a : a + 1, :, sf - 4 * a : sf - 4 * a + n])
+                sf += n
+
+        XR = 2 * PACK * L
+        XG = 2 * XCOLS * PACK
+        xts = []
+        for j in range(2):
+            xt = w2p.tile([P, CH], BF16, name="w2", align_bytes=64)
+            xts.append(xt)
+            for i in range(2):
+                g = 2 * j + i
+                dst = xt[:, i * PACK * L : (i + 1) * PACK * L]
+                if g == LASTG:
+                    nc.sync.dma_start(out=dst, in_=xva[g])
+                else:
+                    nc.sync.dma_start(out=dst.rearrange("p (h w) -> p h w", h=2), in_=xv[g])
         load(0, PIECES)
         load(1, PIECES)
-        load(2, 1)
+        for c in range(2, RAWB):
+            load(c, 1)
 
         mp = HALF // PIECES
 
@@ -103,45 +147,54 @@ def tile_partiallyunsharedconv1d_pa_kernel(tc, x, weight, conv_bias_param, out):
             else:
                 regroup(False, c, PRE_VQ, QUADS, i * mp, (i + 1) * mp)
 
-        xg = keep.tile([P, GROUPS, EXT, A, PACK], BF16, align_bytes=64)
-        nc.vector.memset(xg[:, :, 0:R, 0:1, :], 0.0)
-        nc.vector.memset(xg[:, :, 2 * R : EXT, A - 1 : A, :], 0.0)
         xc = keep.tile([P, GROUPS * XCOLS], U32, align_bytes=64)
         xs = keep.tile([P, GROUPS * XCOLS], U8, align_bytes=64)
-        for g in range(GROUPS):
-            src = xraw[:, g].rearrange("p j (a r) -> p r a j", r=R)
-            if g < 2:
-                nc.vector.tensor_copy(out=xg[:, g, R : 2 * R], in_=src)
-            else:
-                nc.scalar.copy(out=xg[:, g, R : 2 * R], in_=src)
+        xgs = [xt[:, XR : XR + XG].rearrange("p (g r a j) -> p g r a j", g=2, r=EXT, j=PACK) for xt in xts]
+
+        def x_base(j):
+            nc.vector.memset(xgs[j][:, :, 0:R, 0:1, :], 0.0)
+            nc.vector.memset(xgs[j][:, :, 2 * R : EXT, A - 1 : A, :], 0.0)
+            for i in range(2):
+                src = xts[j][:, i * PACK * L : (i + 1) * PACK * L].rearrange("p (t a r) -> p r a t", t=PACK, r=R)
+                copy(j == 0, xgs[j][:, i, R : 2 * R], src)
+
+        def x_shift(j):
+            mid = xgs[j][:, :, R : 2 * R].rearrange("p g r a j -> p g r (a j)")
+            low = xgs[j][:, :, 0:R].rearrange("p g r a j -> p g r (a j)")
+            high = xgs[j][:, :, 2 * R : EXT].rearrange("p g r a j -> p g r (a j)")
+            nc.vector.tensor_copy(out=low[:, :, :, PACK:], in_=mid[:, :, :, : (A - 1) * PACK])
+            nc.vector.tensor_copy(out=high[:, :, :, : (A - 1) * PACK], in_=mid[:, :, :, PACK:])
+
+        def x_quantise(j, c0, n):
+            nc.vector.quantize_mx(
+                out=xc[:, 2 * j * XCOLS + c0 : 2 * j * XCOLS + c0 + n].bitcast(FP8X4),
+                scales=xs[:, 2 * j * XCOLS + c0 : 2 * j * XCOLS + c0 + n],
+                in_=xts[j][:, XR + PACK * c0 : XR + PACK * (c0 + n)],
+            )
+
+        x_base(0)
+        x_base(1)
         for k in range(2 * PIECES):
             first_pieces(False, k)
         first_pieces(True, 0)
-        mid = xg[:, :, R : 2 * R].rearrange("p g r a j -> p g r (a j)")
-        low = xg[:, :, 0:R].rearrange("p g r a j -> p g r (a j)")
-        high = xg[:, :, 2 * R : EXT].rearrange("p g r a j -> p g r (a j)")
-        nc.vector.tensor_copy(out=low[:, :, :, PACK:], in_=mid[:, :, :, : (A - 1) * PACK])
-        nc.vector.tensor_copy(out=high[:, :, :, : (A - 1) * PACK], in_=mid[:, :, :, PACK:])
+        x_shift(0)
         first_pieces(True, 1)
-        xflat = xg[:].rearrange("p g r a j -> p (g r a j)")
-        for c in range(3):
-            nc.vector.quantize_mx(
-                out=xc[:, c * 1024 : (c + 1) * 1024].bitcast(FP8X4),
-                scales=xs[:, c * 1024 : (c + 1) * 1024],
-                in_=xflat[:, c * 4096 : (c + 1) * 4096],
-            )
-            first_pieces(True, 2 + c)
+        x_shift(1)
         bias_f = keep.tile([P, GROUPS * NSEG], F32)
         nc.vector.tensor_copy(out=bias_f[:], in_=bias_bf[:])
-        for k in range(5, 2 * PIECES):
+        for k in range(2, 2 * PIECES):
             first_pieces(True, k)
-        load(3, 1)
-        load(4, 1)
+        for j in range(2):
+            x_quantise(j, 0, 1024)
+            x_quantise(j, 1024, 512)
+        load(RAWB, 1)
+        load(RAWB + 1, 1)
 
         pts = {}
         grps = {}
         cods = {}
         accs = {}
+        osbs = {}
 
         def transposes(n):
             g, a = divmod(n, QUADS)
@@ -159,11 +212,7 @@ def tile_partiallyunsharedconv1d_pa_kernel(tc, x, weight, conv_bias_param, out):
                 grps[n] = grp
             half = CO * PACK
             dst = grps[n][:].bitcast(F32)[:, b * half : (b + 1) * half].rearrange("p (s o h) -> p s o h", s=2, h=2)
-            src = pts[(n, b)][:].rearrange("p s h o -> p s o h")
-            if on_vector:
-                nc.vector.tensor_copy(out=dst, in_=src)
-            else:
-                nc.scalar.copy(out=dst, in_=src)
+            copy(on_vector, dst, pts[(n, b)][:].rearrange("p s h o -> p s o h"))
 
         def quantise(n):
             t, j = divmod(n, BURST)
@@ -172,34 +221,46 @@ def tile_partiallyunsharedconv1d_pa_kernel(tc, x, weight, conv_bias_param, out):
                 ws = codp.tile([P, BURST * 4 * CO], U8, name="ws", align_bytes=64)
                 cods[t] = (wc, ws)
             wc, ws = cods[t]
-            w = 4 * CO
-            nc.vector.quantize_mx(
-                out=wc[:, j * w : (j + 1) * w].bitcast(FP8X4),
-                scales=ws[:, j * w : (j + 1) * w],
-                in_=grps[n][:],
-            )
+            c0 = j * 4 * CO
+            if n < TSTEPS:
+                parts = [grps[n][:]]
+            else:
+                parts = []
+                sf = 4 * (n - TSTEPS)
+                while sf < 4 * (n - TSTEPS) + 4:
+                    k, r0 = divmod(sf, ROWS)
+                    m = min(4 * (n - TSTEPS) + 4 - sf, ROWS - r0)
+                    parts.append(gas[k][:, r0 : r0 + m, :].rearrange("p s m -> p (s m)"))
+                    sf += m
+            w = 4 * CO // len(parts)
+            for i, part in enumerate(parts):
+                nc.vector.quantize_mx(
+                    out=wc[:, c0 + i * w : c0 + (i + 1) * w].bitcast(FP8X4),
+                    scales=ws[:, c0 + i * w : c0 + (i + 1) * w],
+                    in_=part,
+                )
 
-        def burst(t, j0, j1):
-            g, b = divmod(t, QUADS // BURST)
+        def passes(n):
+            t, j = divmod(n, BURST)
+            g, a = divmod(n, QUADS)
             wc, ws = cods[t]
-            for i in range(j0 * 4, j1 * 4):
-                s, f = divmod(b * BURST * 4 + i, TAPS)
+            for i in range(4):
+                s, f = divmod(4 * a + i, TAPS)
                 if f == 0 and s % 2 == 0:
                     bank = accp.tile([P, 2 * L], F32, name="bank")
                     accs[(g, s // 2)] = bank
                 acc = accs[(g, s // 2)][:, (s % 2) * L : (s % 2 + 1) * L]
                 x0 = g * XCOLS + A * f
+                c0 = (4 * j + i) * CO
                 nc.tensor.matmul_mx(
                     out=acc,
-                    lhsT=wc[:, i * CO : (i + 1) * CO].bitcast(FP8X4),
-                    lhsT_scale=ws[:, i * CO : (i + 1) * CO],
+                    lhsT=wc[:, c0 : c0 + CO].bitcast(FP8X4),
+                    lhsT_scale=ws[:, c0 : c0 + CO],
                     rhs=xc[:, x0 : x0 + L].bitcast(FP8X4),
                     rhs_scale=xs[:, x0 : x0 + L],
                     start=(f == 0),
                     stop=(f == TAPS - 1),
                 )
-
-        osbs = {}
 
         def finish(g, part):
             if part == 0:
@@ -214,35 +275,56 @@ def tile_partiallyunsharedconv1d_pa_kernel(tc, x, weight, conv_bias_param, out):
                     scalar1=bias_f[:, g * NSEG + s : g * NSEG + s + 1],
                 )
             if part == 1:
-                nc.sync.dma_start(out=ov[g], in_=osbs[g][:])
+                if g == LASTG:
+                    nc.sync.dma_start(out=ov[g], in_=osbs[g][:])
+                else:
+                    nc.gpsimd.dma_start(out=ov[g], in_=osbs[g][:])
 
+        def units(u0, u1):
+            u = u0
+            while u < u1:
+                c, q = divmod(u, QUADS)
+                c += 2
+                on_vector = (u % (2 * QUADS)) not in S_UNITS
+                n = 1
+                if u + 1 < u1 and q + 1 < QUADS and c < 2 * LASTG and on_vector and ((u + 1) % (2 * QUADS)) not in S_UNITS:
+                    n = 2
+                if c < 2 * LASTG:
+                    regroup(on_vector, c, q, q + n, 0, HALF)
+                else:
+                    regroup_last(on_vector, c - 2 * LASTG, q)
+                if q + n == QUADS and c + RAWB < 2 * GROUPS:
+                    load(c + RAWB, 1)
+                u += n
+
+        UNITS = (2 * GROUPS - 3) * QUADS
         for n in range(LEAD):
             transposes(n)
-        for n in range(STEPS + 1):
-            g, a = divmod(n, QUADS)
-            if n + LEAD < STEPS:
+        for n in range(TSTEPS + 1):
+            if n + LEAD < TSTEPS:
                 transposes(n + LEAD)
-            if n < STEPS:
-                last = g == GROUPS - 1
+            if n < TSTEPS:
                 evacuate(n, 0, False)
-                if not (last and a in V_EVAC_LAST):
-                    evacuate(n, 1, False)
-                if not last:
-                    for u in (2 * a, 2 * a + 1):
-                        h, q = divmod(u, QUADS)
-                        regroup(u not in S_UNITS, 2 * (g + 1) + h, q, q + 1, 0, HALF)
-                        if q == QUADS - 1 and 2 * (g + 1) + h + 3 < 2 * GROUPS:
-                            load(2 * (g + 1) + h + 3, 1)
-                if last and a in V_EVAC_LAST:
-                    evacuate(n, 1, True)
+                evacuate(n, 1, n in V_EVAC)
+                units(max(2 * n - SHIFT, 0), min(2 * n + 2 - SHIFT, UNITS))
             if n > 0:
                 quantise(n - 1)
                 if n % QUADS == 2 and n > 2:
                     finish(n // QUADS - 1, 0)
                     finish(n // QUADS - 1, 1)
-                if n == STEPS - 2:
-                    finish(GROUPS - 1, 0)
             if n > 1:
-                burst((n - 2) // BURST, (n - 2) % BURST, (n - 2) % BURST + 1)
-        burst((STEPS - 1) // BURST, (STEPS - 1) % BURST, (STEPS - 1) % BURST + 1)
-        finish(GROUPS - 1, 1)
+                passes(n - 2)
+        passes(TSTEPS - 1)
+        for a in S_TAIL:
+            regroup_last(False, 1, a)
+        for a in range(QUADS):
+            if a not in S_TAIL:
+                regroup_last(True, 1, a)
+            quantise(TSTEPS + a)
+            if a == 0:
+                finish(LASTG - 1, 0)
+                finish(LASTG - 1, 1)
+            passes(TSTEPS + a)
+            if a == 5:
+                finish(LASTG, 0)
+        finish(LASTG, 1)

@@ -247,7 +247,10 @@ def tile_partiallyunsharedconv1d_pa_kernel(tc, x, weight, conv_bias_param, out):
             for i in range(4):
                 s, f = divmod(4 * a + i, TAPS)
                 if f == 0 and s % 2 == 0:
-                    bank = accp.tile([P, 2 * L], F32, name="bank")
+                    if g == LASTG:
+                        bank = ptp.tile([P, 2 * L], F32, name="pt")
+                    else:
+                        bank = accp.tile([P, 2 * L], F32, name="bank")
                     accs[(g, s // 2)] = bank
                 acc = accs[(g, s // 2)][:, (s % 2) * L : (s % 2 + 1) * L]
                 x0 = g * XCOLS + A * f
@@ -275,10 +278,7 @@ def tile_partiallyunsharedconv1d_pa_kernel(tc, x, weight, conv_bias_param, out):
                     scalar1=bias_f[:, g * NSEG + s : g * NSEG + s + 1],
                 )
             if part == 1:
-                if g == LASTG:
-                    nc.sync.dma_start(out=ov[g], in_=osbs[g][:])
-                else:
-                    nc.gpsimd.dma_start(out=ov[g], in_=osbs[g][:])
+                nc.sync.dma_start(out=ov[g], in_=osbs[g][:])
 
         def units(u0, u1):
             u = u0
@@ -315,16 +315,14 @@ def tile_partiallyunsharedconv1d_pa_kernel(tc, x, weight, conv_bias_param, out):
             if n > 1:
                 passes(n - 2)
         passes(TSTEPS - 1)
-        for a in S_TAIL:
-            regroup_last(False, 1, a)
         for a in range(QUADS):
-            if a not in S_TAIL:
-                regroup_last(True, 1, a)
+            regroup_last(a not in S_TAIL, 1, a)
+        for a in range(QUADS):
             quantise(TSTEPS + a)
-            if a == 0:
+            passes(TSTEPS + a)
+            if a == 2:
                 finish(LASTG - 1, 0)
                 finish(LASTG - 1, 1)
-            passes(TSTEPS + a)
-            if a == 5:
+            if a == 6:
                 finish(LASTG, 0)
         finish(LASTG, 1)

@@ -64,6 +64,10 @@ def tile_partiallyunsharedconv1d_pa_kernel(tc, x, weight, conv_bias_param, out):
         ptp = ctx.enter_context(tc.psum_pool(name="ptp", bufs=6))
         accp = ctx.enter_context(tc.psum_pool(name="accp", bufs=2))
 
+        cold = keep.tile([P, 1], F32)
+        warm = keep.tile([P, 1], F32)
+        nc.vector.memset(cold[:], 0.0)
+        nc.scalar.activation(out=warm[:], in_=cold[:], func=mybir.ActivationFunctionType.Identity)
         ident = keep.tile([P, P], F32)
         make_identity(nc, ident[:])
         bias_bf = keep.tile([P, GROUPS * NSEG], BF16)
@@ -265,18 +269,27 @@ def tile_partiallyunsharedconv1d_pa_kernel(tc, x, weight, conv_bias_param, out):
                     stop=(f == TAPS - 1),
                 )
 
-        def finish(g, part):
+        def finish(g, part, on_vector=True):
             if part == 0:
                 osb = outp.tile([P, L], F32, name="osb")
                 osbs[g] = osb
             oar = osbs[g][:].rearrange("p (a r) -> p a r", r=R)
             for s, a0, a1, r0 in CUTS[3 * part : 3 * part + 3]:
                 acc = accs[(g, s // 2)][:, (s % 2) * L : (s % 2 + 1) * L].rearrange("p (r a) -> p a r", r=R)
-                nc.vector.tensor_scalar_add(
-                    out=oar[:, a0:a1, r0:R],
-                    in0=acc[:, a0:a1, r0:R],
-                    scalar1=bias_f[:, g * NSEG + s : g * NSEG + s + 1],
-                )
+                if on_vector:
+                    nc.vector.tensor_scalar_add(
+                        out=oar[:, a0:a1, r0:R],
+                        in0=acc[:, a0:a1, r0:R],
+                        scalar1=bias_f[:, g * NSEG + s : g * NSEG + s + 1],
+                    )
+                else:
+                    nc.scalar.activation(
+                        out=oar[:, a0:a1, r0:R],
+                        in_=acc[:, a0:a1, r0:R],
+                        func=mybir.ActivationFunctionType.Identity,
+                        bias=bias_f[:, g * NSEG + s : g * NSEG + s + 1],
+                        scale=1.0,
+                    )
             if part == 1:
                 nc.sync.dma_start(out=ov[g], in_=osbs[g][:])
 
@@ -320,9 +333,8 @@ def tile_partiallyunsharedconv1d_pa_kernel(tc, x, weight, conv_bias_param, out):
         for a in range(QUADS):
             quantise(TSTEPS + a)
             passes(TSTEPS + a)
-            if a == 2:
-                finish(LASTG - 1, 0)
-                finish(LASTG - 1, 1)
             if a == 6:
-                finish(LASTG, 0)
-        finish(LASTG, 1)
+                finish(LASTG, 0, False)
+                finish(LASTG - 1, 0, False)
+                finish(LASTG - 1, 1, False)
+        finish(LASTG, 1, False)

@@ -8,6 +8,7 @@ BF16 = mybir.dt.bfloat16
 F32 = mybir.dt.float32
 U32 = mybir.dt.uint32
 U8 = mybir.dt.uint8
+I32 = mybir.dt.int32
 
 P = 128
 GROUPS = 4
@@ -36,7 +37,7 @@ SHIFT = 4
 S_UNITS = (3, 7, 12, 16)
 S_TAIL = (1, 2, 4, 5, 7, 8)
 PRE_VQ = 5
-V_EVAC = (25, 26)
+V_EVAC = ()
 
 CUTS = ((0, 0, 15, 0), (1, 15, 29, 0), (1, 14, 15, 2), (2, 29, 44, 0), (3, 44, 64, 0), (3, 43, 44, 2))
 
@@ -125,11 +126,11 @@ def tile_partiallyunsharedconv1d_pa_kernel(tc, x, weight, conv_bias_param, out):
                 sf += n
 
         XR = 2 * PACK * L
-        XG = 2 * XCOLS * PACK
-        xts = []
-        for j in range(2):
+        xts = {}
+
+        def load_x(j):
             xt = w2p.tile([P, CH], BF16, name="w2", align_bytes=64)
-            xts.append(xt)
+            xts[j] = xt
             for i in range(2):
                 g = 2 * j + i
                 dst = xt[:, i * PACK * L : (i + 1) * PACK * L]
@@ -137,7 +138,10 @@ def tile_partiallyunsharedconv1d_pa_kernel(tc, x, weight, conv_bias_param, out):
                     nc.sync.dma_start(out=dst, in_=xva[g])
                 else:
                     nc.sync.dma_start(out=dst.rearrange("p (h w) -> p h w", h=2), in_=xv[g])
+
+        load_x(0)
         load(0, PIECES)
+        load_x(1)
         load(1, PIECES)
         for c in range(2, RAWB):
             load(c, 1)
@@ -153,44 +157,44 @@ def tile_partiallyunsharedconv1d_pa_kernel(tc, x, weight, conv_bias_param, out):
 
         xc = keep.tile([P, GROUPS * XCOLS], U32, align_bytes=64)
         xs = keep.tile([P, GROUPS * XCOLS], U8, align_bytes=64)
-        xgs = [xt[:, XR : XR + XG].rearrange("p (g r a j) -> p g r a j", g=2, r=EXT, j=PACK) for xt in xts]
+        xci = xc[:].bitcast(I32).rearrange("p (g r a) -> p g r a", g=GROUPS, r=EXT)
+        xsi = xs[:].rearrange("p (g r a) -> p g r a", g=GROUPS, r=EXT)
+        for plane in (xci, xsi):
+            nc.vector.memset(plane[:, :, 0:R, 0:1], 0)
+            nc.vector.memset(plane[:, :, 2 * R : EXT, A - 1 : A], 0)
 
-        def x_base(j):
-            nc.vector.memset(xgs[j][:, :, 0:R, 0:1, :], 0.0)
-            nc.vector.memset(xgs[j][:, :, 2 * R : EXT, A - 1 : A, :], 0.0)
+        def x_base(j, on_vector):
             for i in range(2):
                 src = xts[j][:, i * PACK * L : (i + 1) * PACK * L].rearrange("p (t a r) -> p r a t", t=PACK, r=R)
-                copy(j == 0, xgs[j][:, i, R : 2 * R], src)
+                dst = xts[j][:, XR + i * PACK * L : XR + (i + 1) * PACK * L].rearrange("p (r a t) -> p r a t", r=R, t=PACK)
+                copy(on_vector, dst, src)
+
+        def x_quantise(j):
+            for i in range(2):
+                c0 = (2 * j + i) * XCOLS + R * A
+                nc.vector.quantize_mx(
+                    out=xc[:, c0 : c0 + R * A].bitcast(FP8X4),
+                    scales=xs[:, c0 : c0 + R * A],
+                    in_=xts[j][:, XR + i * PACK * L : XR + (i + 1) * PACK * L],
+                )
 
         def x_shift(j):
-            mid = xgs[j][:, :, R : 2 * R].rearrange("p g r a j -> p g r (a j)")
-            low = xgs[j][:, :, 0:R].rearrange("p g r a j -> p g r (a j)")
-            high = xgs[j][:, :, 2 * R : EXT].rearrange("p g r a j -> p g r (a j)")
-            nc.vector.tensor_copy(out=low[:, :, :, PACK:], in_=mid[:, :, :, : (A - 1) * PACK])
-            nc.vector.tensor_copy(out=high[:, :, :, : (A - 1) * PACK], in_=mid[:, :, :, PACK:])
+            for plane in (xci[:, 2 * j : 2 * j + 2], xsi[:, 2 * j : 2 * j + 2]):
+                nc.vector.tensor_copy(out=plane[:, :, 0:R, 1:A], in_=plane[:, :, R : 2 * R, 0 : A - 1])
+                nc.vector.tensor_copy(out=plane[:, :, 2 * R : EXT, 0 : A - 1], in_=plane[:, :, R : 2 * R, 1:A])
 
-        def x_quantise(j, c0, n):
-            nc.vector.quantize_mx(
-                out=xc[:, 2 * j * XCOLS + c0 : 2 * j * XCOLS + c0 + n].bitcast(FP8X4),
-                scales=xs[:, 2 * j * XCOLS + c0 : 2 * j * XCOLS + c0 + n],
-                in_=xts[j][:, XR + PACK * c0 : XR + PACK * (c0 + n)],
-            )
-
-        x_base(0)
-        x_base(1)
+        x_base(0, True)
+        x_quantise(0)
+        x_shift(0)
         for k in range(2 * PIECES):
             first_pieces(False, k)
-        first_pieces(True, 0)
-        x_shift(0)
-        first_pieces(True, 1)
-        x_shift(1)
+        for k in range(2 * PIECES):
+            first_pieces(True, k)
         bias_f = keep.tile([P, GROUPS * NSEG], F32)
         nc.vector.tensor_copy(out=bias_f[:], in_=bias_bf[:])
-        for k in range(2, 2 * PIECES):
-            first_pieces(True, k)
-        for j in range(2):
-            x_quantise(j, 0, 1024)
-            x_quantise(j, 1024, 512)
+        x_base(1, True)
+        x_quantise(1)
+        x_shift(1)
         load(RAWB, 1)
         load(RAWB + 1, 1)
 

@@ -34,9 +34,13 @@ CH = HALF * SF
 RAWB = 4
 SHIFT = 4
 
-S_UNITS = (3, 7, 12, 16)
-S_TAIL = (1, 2, 4, 5, 7, 8)
-PRE_VQ = 5
+KINDS = "HCC"
+S_UNITS = {"C": (1, 5, 9, 12, 16), "D": ()}
+S_FIRST = ((5, 6, 7, 8), (6, 7, 8))
+PIECES_LAST = ((0, 48), (48, 16))
+S_TAIL = ((1, 2, 4, 5, 7, 8), ())
+SPLIT_Q = False
+Q_AT = 0
 V_EVAC = ()
 
 CUTS = ((0, 0, 15, 0), (1, 15, 29, 0), (1, 14, 15, 2), (2, 29, 44, 0), (3, 44, 64, 0), (3, 43, 44, 2))
@@ -47,6 +51,9 @@ FLOPS = 2 * GROUPS * CO * CI * TAPS * L
 def tile_partiallyunsharedconv1d_pa_kernel(tc, x, weight, conv_bias_param, out):
     nc = tc.nc
     xv = x.rearrange("b d k (h p e) l -> (b d k) p h (e l)", h=2, e=2)
+    xd = x.rearrange("b d k (j p) l -> (b d k) p j l", j=PACK)
+    wd = weight.rearrange("d k o (j i) s u f -> (d k) (o j) (i s u f)", j=PACK)
+    wh = weight.rearrange("d k o (h i) s u f -> (d k) (o h) (i s u f)", h=2)
     xva = x.rearrange("b d k (p j) l -> (b d k) p (j l)", j=PACK)
     wv = weight.rearrange("d k o i s u f -> (d k) o (i s u f)")
     wva = weight.rearrange("d k o (p j) s u f -> (d k) p o (j s u f)", j=PACK)
@@ -59,7 +66,7 @@ def tile_partiallyunsharedconv1d_pa_kernel(tc, x, weight, conv_bias_param, out):
         keep = ctx.enter_context(tc.tile_pool(name="keep", bufs=1))
         rawp = ctx.enter_context(tc.tile_pool(name="rawp", bufs=RAWB))
         w2p = ctx.enter_context(tc.tile_pool(name="w2p", bufs=4))
-        grpp = ctx.enter_context(tc.tile_pool(name="grpp", bufs=4))
+        grpp = ctx.enter_context(tc.tile_pool(name="grpp", bufs=11))
         codp = ctx.enter_context(tc.tile_pool(name="codp", bufs=4))
         outp = ctx.enter_context(tc.tile_pool(name="outp", bufs=4))
         ptp = ctx.enter_context(tc.psum_pool(name="ptp", bufs=6))
@@ -71,6 +78,8 @@ def tile_partiallyunsharedconv1d_pa_kernel(tc, x, weight, conv_bias_param, out):
         nc.scalar.activation(out=warm[:], in_=cold[:], func=mybir.ActivationFunctionType.Identity)
         ident = keep.tile([P, P], F32)
         make_identity(nc, ident[:])
+        ident_b = keep.tile([P, P], BF16)
+        nc.vector.tensor_copy(out=ident_b[:], in_=ident[:])
         bias_bf = keep.tile([P, GROUPS * NSEG], BF16)
         nc.gpsimd.dma_start(out=bias_bf[:].rearrange("o (g s) -> o g s", s=NSEG), in_=bv)
 
@@ -83,17 +92,23 @@ def tile_partiallyunsharedconv1d_pa_kernel(tc, x, weight, conv_bias_param, out):
             g, h = divmod(c, 2)
             if g == LASTG:
                 half = CO // 2
-                nc.sync.dma_start(
-                    out=raw[:].rearrange("p (o e) -> p o e", o=half),
-                    in_=wva[g][:, h * half : (h + 1) * half, :],
-                )
+                for o0, n in PIECES_LAST if h == 1 else ((0, half),):
+                    nc.sync.dma_start(
+                        out=raw[:, o0 * PACK * SF : (o0 + n) * PACK * SF].rearrange("p (o e) -> p o e", o=n),
+                        in_=wva[g][:, h * half + o0 : h * half + o0 + n, :],
+                    )
+            elif KINDS[g] == "D":
+                for i in range(2):
+                    r0 = (2 * h + i) * P
+                    nc.sync.dma_start(out=raw[:, i * CH // 2 : (i + 1) * CH // 2], in_=wd[g][r0 : r0 + P, :])
             else:
                 w = CH // pieces
                 for i in range(pieces):
-                    nc.sync.dma_start(
-                        out=raw[:, i * w : (i + 1) * w],
-                        in_=wv[g][:, h * CH + i * w : h * CH + (i + 1) * w],
-                    )
+                    if KINDS[g] == "H":
+                        src = wh[g][h * P : (h + 1) * P, i * w : (i + 1) * w]
+                    else:
+                        src = wv[g][:, h * CH + i * w : h * CH + (i + 1) * w]
+                    nc.sync.dma_start(out=raw[:, i * w : (i + 1) * w], in_=src)
 
         def copy(on_vector, dst, src):
             if on_vector:
@@ -105,6 +120,11 @@ def tile_partiallyunsharedconv1d_pa_kernel(tc, x, weight, conv_bias_param, out):
             if c not in w2s:
                 w2 = w2p.tile([P, SF, HALF], BF16, name="w2", align_bytes=64)
                 w2s[c] = w2
+            if KINDS[c // 2] == "D":
+                words = w2s[c][:].rearrange("p f m -> p (f m)").bitcast(F32).rearrange("p (m t i) -> p t i m", m=SF // 2, t=2)
+                raw = raws[c][:].bitcast(F32).rearrange("p (t i m) -> p t i m", t=2, m=SF // 2)
+                copy(on_vector, words[:, :, :, 2 * q0 : 2 * q1], raw[:, :, :, 2 * q0 : 2 * q1])
+                return
             src = raws[c][:, m0 * SF : m1 * SF].rearrange("p (m a q) -> p a m q", a=QUADS, q=4)
             dst = w2s[c][:, :, m0:m1].rearrange("p (a q) m -> p a m q", q=4)
             copy(on_vector, dst[:, q0:q1], src[:, q0:q1])
@@ -112,8 +132,9 @@ def tile_partiallyunsharedconv1d_pa_kernel(tc, x, weight, conv_bias_param, out):
         gas = {}
         ROWS = SF // 2
 
-        def regroup_last(on_vector, h, a):
-            src = raws[2 * LASTG + h][:].rearrange("p (m a q) -> p a m q", a=QUADS, q=4)
+        def regroup_last(on_vector, h, a, o0=0, n_o=CO // 2):
+            m0, m1 = o0 * PACK, (o0 + n_o) * PACK
+            src = raws[2 * LASTG + h][:, m0 * SF : m1 * SF].rearrange("p (m a q) -> p a m q", a=QUADS, q=4)
             sf = 4 * a
             while sf < 4 * a + 4:
                 t, r0 = divmod(sf, ROWS)
@@ -121,7 +142,7 @@ def tile_partiallyunsharedconv1d_pa_kernel(tc, x, weight, conv_bias_param, out):
                 if t not in gas:
                     ga = w2p.tile([P, ROWS, CO * PACK], BF16, name="w2", align_bytes=64)
                     gas[t] = ga
-                dst = gas[t][:, r0 : r0 + n, h * HALF : (h + 1) * HALF].rearrange("p (a q) m -> p a m q", q=n)
+                dst = gas[t][:, r0 : r0 + n, h * HALF + m0 : h * HALF + m1].rearrange("p (a q) m -> p a m q", q=n)
                 copy(on_vector, dst, src[:, a : a + 1, :, sf - 4 * a : sf - 4 * a + n])
                 sf += n
 
@@ -136,24 +157,25 @@ def tile_partiallyunsharedconv1d_pa_kernel(tc, x, weight, conv_bias_param, out):
                 dst = xt[:, i * PACK * L : (i + 1) * PACK * L]
                 if g == LASTG:
                     nc.sync.dma_start(out=dst, in_=xva[g])
+                elif KINDS[g] == "D":
+                    nc.sync.dma_start(out=dst.rearrange("p (j l) -> p j l", j=PACK), in_=xd[g])
                 else:
                     nc.sync.dma_start(out=dst.rearrange("p (h w) -> p h w", h=2), in_=xv[g])
 
-        load_x(0)
         load(0, PIECES)
-        load_x(1)
+        load_x(0)
         load(1, PIECES)
+        load_x(1)
         for c in range(2, RAWB):
             load(c, 1)
 
         mp = HALF // PIECES
 
-        def first_pieces(on_vector, k):
-            c, i = divmod(k, PIECES)
-            if on_vector:
-                regroup(True, c, 0, PRE_VQ, i * mp, (i + 1) * mp)
-            else:
-                regroup(False, c, PRE_VQ, QUADS, i * mp, (i + 1) * mp)
+        def first_pieces(on_vector, c):
+            for i in range(PIECES):
+                for a in range(QUADS):
+                    if (a in S_FIRST[c]) != on_vector:
+                        regroup(on_vector, c, a, a + 1, i * mp, (i + 1) * mp)
 
         xc = keep.tile([P, GROUPS * XCOLS], U32, align_bytes=64)
         xs = keep.tile([P, GROUPS * XCOLS], U8, align_bytes=64)
@@ -183,20 +205,15 @@ def tile_partiallyunsharedconv1d_pa_kernel(tc, x, weight, conv_bias_param, out):
                 nc.vector.tensor_copy(out=plane[:, :, 0:R, 1:A], in_=plane[:, :, R : 2 * R, 0 : A - 1])
                 nc.vector.tensor_copy(out=plane[:, :, 2 * R : EXT, 0 : A - 1], in_=plane[:, :, R : 2 * R, 1:A])
 
+        bias_f = keep.tile([P, GROUPS * NSEG], F32)
+        first_pieces(True, 0)
+        first_pieces(False, 0)
         x_base(0, True)
         x_quantise(0)
         x_shift(0)
-        for k in range(2 * PIECES):
-            first_pieces(False, k)
-        for k in range(2 * PIECES):
-            first_pieces(True, k)
-        bias_f = keep.tile([P, GROUPS * NSEG], F32)
         nc.vector.tensor_copy(out=bias_f[:], in_=bias_bf[:])
-        x_base(1, True)
-        x_quantise(1)
-        x_shift(1)
+        first_pieces(True, 1)
         load(RAWB, 1)
-        load(RAWB + 1, 1)
 
         pts = {}
         grps = {}
@@ -204,9 +221,24 @@ def tile_partiallyunsharedconv1d_pa_kernel(tc, x, weight, conv_bias_param, out):
         accs = {}
         osbs = {}
 
-        def transposes(n):
+        def transposes(n, halves=(0, 1)):
             g, a = divmod(n, QUADS)
-            for b in range(2):
+            for b in halves:
+                if KINDS[g] == "H":
+                    pt = ptp.tile([P, 4, P], F32, name="pt")
+                    pts[(n, b)] = pt
+                    for s in range(4):
+                        nc.tensor.transpose(pt[:, s, :], w2s[2 * g + b][:, 4 * a + s, :].bitcast(F32), ident[:])
+                    continue
+                if KINDS[g] == "D":
+                    pt = ptp.tile([P, 4, 2, P], BF16, name="pt")
+                    pts[(n, b)] = pt
+                    src = w2s[2 * g + b][:].rearrange("p (m v) i -> p m (v i)", v=2)
+                    src = src.rearrange("p m (t i w) -> p m w t i", t=2, w=2)
+                    for s in range(4):
+                        for t in range(2):
+                            nc.tensor.transpose(pt[:, s, t, :], src[:, 2 * a + s // 2, s % 2, t, :], ident_b[:])
+                    continue
                 pt = ptp.tile([P, 2, 2, CO], F32, name="pt")
                 pts[(n, b)] = pt
                 for s in range(2):
@@ -215,9 +247,18 @@ def tile_partiallyunsharedconv1d_pa_kernel(tc, x, weight, conv_bias_param, out):
                         nc.tensor.transpose(pt[:, s, h, :], w2s[2 * g + h][:, sf, :].bitcast(F32), ident[:])
 
         def evacuate(n, b, on_vector):
-            if b == 0:
+            if n not in grps:
                 grp = grpp.tile([P, 4 * CO * PACK], BF16, name="grp", align_bytes=64)
                 grps[n] = grp
+            half = CO // 2 * PACK
+            if KINDS[n // QUADS] == "H":
+                dst = grps[n][:].bitcast(F32).rearrange("p (s m) -> p s m", s=4)[:, :, b * P : (b + 1) * P]
+                copy(on_vector, dst, pts[(n, b)][:])
+                return
+            if KINDS[n // QUADS] == "D":
+                dst = grps[n][:].rearrange("p (s m) -> p s m", s=4)[:, :, b * half : (b + 1) * half]
+                copy(on_vector, dst, pts[(n, b)][:].rearrange("p s t o -> p s (t o)"))
+                return
             half = CO * PACK
             dst = grps[n][:].bitcast(F32)[:, b * half : (b + 1) * half].rearrange("p (s o h) -> p s o h", s=2, h=2)
             copy(on_vector, dst, pts[(n, b)][:].rearrange("p s h o -> p s o h"))
@@ -246,6 +287,23 @@ def tile_partiallyunsharedconv1d_pa_kernel(tc, x, weight, conv_bias_param, out):
                     out=wc[:, c0 + i * w : c0 + (i + 1) * w].bitcast(FP8X4),
                     scales=ws[:, c0 + i * w : c0 + (i + 1) * w],
                     in_=part,
+                )
+
+        def quantise_half(n, h):
+            t, j = divmod(n, BURST)
+            if t not in cods:
+                wc = codp.tile([P, BURST * 4 * CO], U32, name="wc", align_bytes=64)
+                ws = codp.tile([P, BURST * 4 * CO], U8, name="ws", align_bytes=64)
+                cods[t] = (wc, ws)
+            wc, ws = cods[t]
+            for i in range(4):
+                sf = 4 * (n - TSTEPS) + i
+                c0 = (4 * j + i) * CO + h * CO // 2
+                k, r0 = divmod(sf, ROWS)
+                nc.vector.quantize_mx(
+                    out=wc[:, c0 : c0 + CO // 2].bitcast(FP8X4),
+                    scales=ws[:, c0 : c0 + CO // 2],
+                    in_=gas[k][:, r0, h * HALF : (h + 1) * HALF],
                 )
 
         def passes(n):
@@ -302,9 +360,10 @@ def tile_partiallyunsharedconv1d_pa_kernel(tc, x, weight, conv_bias_param, out):
             while u < u1:
                 c, q = divmod(u, QUADS)
                 c += 2
-                on_vector = (u % (2 * QUADS)) not in S_UNITS
+                kind = KINDS[c // 2] if c < 2 * LASTG else "C"
+                on_vector = (u % (2 * QUADS)) not in S_UNITS[kind]
                 n = 1
-                if u + 1 < u1 and q + 1 < QUADS and c < 2 * LASTG and on_vector and ((u + 1) % (2 * QUADS)) not in S_UNITS:
+                if u + 1 < u1 and q + 1 < QUADS and c < 2 * LASTG and on_vector and ((u + 1) % (2 * QUADS)) not in S_UNITS[kind]:
                     n = 2
                 if c < 2 * LASTG:
                     regroup(on_vector, c, q, q + n, 0, HALF)
@@ -315,13 +374,26 @@ def tile_partiallyunsharedconv1d_pa_kernel(tc, x, weight, conv_bias_param, out):
                 u += n
 
         UNITS = (2 * GROUPS - 3) * QUADS
+        for n in range(QUADS):
+            transposes(n, (0,))
+            evacuate(n, 0, False)
+        first_pieces(False, 1)
+        load(RAWB + 1, 1)
+        x_base(1, True)
+        x_quantise(1)
+        x_shift(1)
+
+        def turn(n):
+            transposes(n, (1,) if n < QUADS else (0, 1))
+
         for n in range(LEAD):
-            transposes(n)
+            turn(n)
         for n in range(TSTEPS + 1):
             if n + LEAD < TSTEPS:
-                transposes(n + LEAD)
+                turn(n + LEAD)
             if n < TSTEPS:
-                evacuate(n, 0, False)
+                if n >= QUADS:
+                    evacuate(n, 0, False)
                 evacuate(n, 1, n in V_EVAC)
                 units(max(2 * n - SHIFT, 0), min(2 * n + 2 - SHIFT, UNITS))
             if n > 0:
@@ -332,12 +404,21 @@ def tile_partiallyunsharedconv1d_pa_kernel(tc, x, weight, conv_bias_param, out):
             if n > 1:
                 passes(n - 2)
         passes(TSTEPS - 1)
+        for i in range(len(PIECES_LAST) - 1):
+            for a in range(QUADS):
+                regroup_last(a not in S_TAIL[i], 1, a, *PIECES_LAST[i])
+            if SPLIT_Q and i == Q_AT:
+                for a in range(QUADS):
+                    quantise_half(TSTEPS + a, 0)
         for a in range(QUADS):
-            regroup_last(a not in S_TAIL, 1, a)
-        for a in range(QUADS):
-            quantise(TSTEPS + a)
-            passes(TSTEPS + a)
-            if a == 6:
+            regroup_last(a not in S_TAIL[-1], 1, a, *PIECES_LAST[-1])
+            for b in ([a - 1] if a > 0 else []) + ([a] if a == QUADS - 1 else []):
+                if SPLIT_Q:
+                    quantise_half(TSTEPS + b, 1)
+                else:
+                    quantise(TSTEPS + b)
+                passes(TSTEPS + b)
+            if a == 7:
                 finish(LASTG, 0, False)
                 finish(LASTG - 1, 0, False)
                 finish(LASTG - 1, 1, False)

@@ -29,18 +29,15 @@ PIECES = 4
 STEPS = GROUPS * QUADS
 TSTEPS = STEPS - QUADS
 LEAD = 2
-BURST = 3
 CH = HALF * SF
 RAWB = 4
 SHIFT = 4
 
 KINDS = "HCC"
-S_UNITS = {"C": (1, 5, 9, 12, 16), "D": ()}
-S_FIRST = ((5, 6, 7, 8), (6, 7, 8))
+S_UNITS = {"C": (1, 5, 9, 12, 16), "D": (4, 13)}
+V_FIRST = (5, 6)
 PIECES_LAST = ((0, 48), (48, 16))
 S_TAIL = ((1, 2, 4, 5, 7, 8), ())
-SPLIT_Q = False
-Q_AT = 0
 V_EVAC = ()
 
 CUTS = ((0, 0, 15, 0), (1, 15, 29, 0), (1, 14, 15, 2), (2, 29, 44, 0), (3, 44, 64, 0), (3, 43, 44, 2))
@@ -66,8 +63,8 @@ def tile_partiallyunsharedconv1d_pa_kernel(tc, x, weight, conv_bias_param, out):
         keep = ctx.enter_context(tc.tile_pool(name="keep", bufs=1))
         rawp = ctx.enter_context(tc.tile_pool(name="rawp", bufs=RAWB))
         w2p = ctx.enter_context(tc.tile_pool(name="w2p", bufs=4))
-        grpp = ctx.enter_context(tc.tile_pool(name="grpp", bufs=11))
-        codp = ctx.enter_context(tc.tile_pool(name="codp", bufs=4))
+        grpp = ctx.enter_context(tc.tile_pool(name="grpp", bufs=6))
+        codp = ctx.enter_context(tc.tile_pool(name="codp", bufs=5))
         outp = ctx.enter_context(tc.tile_pool(name="outp", bufs=4))
         ptp = ctx.enter_context(tc.psum_pool(name="ptp", bufs=6))
         accp = ctx.enter_context(tc.psum_pool(name="accp", bufs=2))
@@ -93,7 +90,7 @@ def tile_partiallyunsharedconv1d_pa_kernel(tc, x, weight, conv_bias_param, out):
             if g == LASTG:
                 half = CO // 2
                 for o0, n in PIECES_LAST if h == 1 else ((0, half),):
-                    nc.sync.dma_start(
+                    nc.scalar.dma_start(
                         out=raw[:, o0 * PACK * SF : (o0 + n) * PACK * SF].rearrange("p (o e) -> p o e", o=n),
                         in_=wva[g][:, h * half + o0 : h * half + o0 + n, :],
                     )
@@ -172,10 +169,9 @@ def tile_partiallyunsharedconv1d_pa_kernel(tc, x, weight, conv_bias_param, out):
         mp = HALF // PIECES
 
         def first_pieces(on_vector, c):
+            q0, q1 = (0, V_FIRST[c]) if on_vector else (V_FIRST[c], QUADS)
             for i in range(PIECES):
-                for a in range(QUADS):
-                    if (a in S_FIRST[c]) != on_vector:
-                        regroup(on_vector, c, a, a + 1, i * mp, (i + 1) * mp)
+                regroup(on_vector, c, q0, q1, i * mp, (i + 1) * mp)
 
         xc = keep.tile([P, GROUPS * XCOLS], U32, align_bytes=64)
         xs = keep.tile([P, GROUPS * XCOLS], U8, align_bytes=64)
@@ -217,6 +213,7 @@ def tile_partiallyunsharedconv1d_pa_kernel(tc, x, weight, conv_bias_param, out):
 
         pts = {}
         grps = {}
+        pairs = {}
         cods = {}
         accs = {}
         osbs = {}
@@ -246,33 +243,40 @@ def tile_partiallyunsharedconv1d_pa_kernel(tc, x, weight, conv_bias_param, out):
                     for h in range(2):
                         nc.tensor.transpose(pt[:, s, h, :], w2s[2 * g + h][:, sf, :].bitcast(F32), ident[:])
 
+        W = 4 * CO * PACK
+
         def evacuate(n, b, on_vector):
             if n not in grps:
-                grp = grpp.tile([P, 4 * CO * PACK], BF16, name="grp", align_bytes=64)
-                grps[n] = grp
+                grp = grpp.tile([P, 2 * W], BF16, name="grp", align_bytes=64)
+                pairs[n // 2] = grp[:]
+                for i in range(2):
+                    grps[n - n % 2 + i] = grp[:, i * W : (i + 1) * W]
             half = CO // 2 * PACK
             if KINDS[n // QUADS] == "H":
-                dst = grps[n][:].bitcast(F32).rearrange("p (s m) -> p s m", s=4)[:, :, b * P : (b + 1) * P]
+                dst = grps[n].bitcast(F32).rearrange("p (s m) -> p s m", s=4)[:, :, b * P : (b + 1) * P]
                 copy(on_vector, dst, pts[(n, b)][:])
                 return
             if KINDS[n // QUADS] == "D":
-                dst = grps[n][:].rearrange("p (s m) -> p s m", s=4)[:, :, b * half : (b + 1) * half]
+                dst = grps[n].rearrange("p (s m) -> p s m", s=4)[:, :, b * half : (b + 1) * half]
                 copy(on_vector, dst, pts[(n, b)][:].rearrange("p s t o -> p s (t o)"))
                 return
             half = CO * PACK
-            dst = grps[n][:].bitcast(F32)[:, b * half : (b + 1) * half].rearrange("p (s o h) -> p s o h", s=2, h=2)
+            dst = grps[n].bitcast(F32)[:, b * half : (b + 1) * half].rearrange("p (s o h) -> p s o h", s=2, h=2)
             copy(on_vector, dst, pts[(n, b)][:].rearrange("p s h o -> p s o h"))
 
-        def quantise(n):
-            t, j = divmod(n, BURST)
-            if j == 0:
-                wc = codp.tile([P, BURST * 4 * CO], U32, name="wc", align_bytes=64)
-                ws = codp.tile([P, BURST * 4 * CO], U8, name="ws", align_bytes=64)
+        def code_tiles(n):
+            t, j = divmod(n, 2)
+            if t not in cods:
+                wc = codp.tile([P, 2 * 4 * CO], U32, name="wc", align_bytes=64)
+                ws = codp.tile([P, 2 * 4 * CO], U8, name="ws", align_bytes=64)
                 cods[t] = (wc, ws)
-            wc, ws = cods[t]
-            c0 = j * 4 * CO
+            return cods[t], j * 4 * CO
+
+        def quantise(n, quads):
+            (wc, ws), c0 = code_tiles(n)
             if n < TSTEPS:
-                parts = [grps[n][:]]
+                whole = grps[n] if quads == 1 else pairs[n // 2]
+                parts = [whole]
             else:
                 parts = []
                 sf = 4 * (n - TSTEPS)
@@ -281,7 +285,7 @@ def tile_partiallyunsharedconv1d_pa_kernel(tc, x, weight, conv_bias_param, out):
                     m = min(4 * (n - TSTEPS) + 4 - sf, ROWS - r0)
                     parts.append(gas[k][:, r0 : r0 + m, :].rearrange("p s m -> p (s m)"))
                     sf += m
-            w = 4 * CO // len(parts)
+            w = quads * 4 * CO // len(parts)
             for i, part in enumerate(parts):
                 nc.vector.quantize_mx(
                     out=wc[:, c0 + i * w : c0 + (i + 1) * w].bitcast(FP8X4),
@@ -289,27 +293,9 @@ def tile_partiallyunsharedconv1d_pa_kernel(tc, x, weight, conv_bias_param, out):
                     in_=part,
                 )
 
-        def quantise_half(n, h):
-            t, j = divmod(n, BURST)
-            if t not in cods:
-                wc = codp.tile([P, BURST * 4 * CO], U32, name="wc", align_bytes=64)
-                ws = codp.tile([P, BURST * 4 * CO], U8, name="ws", align_bytes=64)
-                cods[t] = (wc, ws)
-            wc, ws = cods[t]
-            for i in range(4):
-                sf = 4 * (n - TSTEPS) + i
-                c0 = (4 * j + i) * CO + h * CO // 2
-                k, r0 = divmod(sf, ROWS)
-                nc.vector.quantize_mx(
-                    out=wc[:, c0 : c0 + CO // 2].bitcast(FP8X4),
-                    scales=ws[:, c0 : c0 + CO // 2],
-                    in_=gas[k][:, r0, h * HALF : (h + 1) * HALF],
-                )
-
         def passes(n):
-            t, j = divmod(n, BURST)
             g, a = divmod(n, QUADS)
-            wc, ws = cods[t]
+            (wc, ws), base = code_tiles(n)
             for i in range(4):
                 s, f = divmod(4 * a + i, TAPS)
                 if f == 0 and s % 2 == 0:
@@ -320,7 +306,7 @@ def tile_partiallyunsharedconv1d_pa_kernel(tc, x, weight, conv_bias_param, out):
                     accs[(g, s // 2)] = bank
                 acc = accs[(g, s // 2)][:, (s % 2) * L : (s % 2 + 1) * L]
                 x0 = g * XCOLS + A * f
-                c0 = (4 * j + i) * CO
+                c0 = base + i * CO
                 nc.tensor.matmul_mx(
                     out=acc,
                     lhsT=wc[:, c0 : c0 + CO].bitcast(FP8X4),
@@ -355,6 +341,8 @@ def tile_partiallyunsharedconv1d_pa_kernel(tc, x, weight, conv_bias_param, out):
             if part == 1:
                 nc.sync.dma_start(out=ov[g], in_=osbs[g][:])
 
+        freed = []
+
         def units(u0, u1):
             u = u0
             while u < u1:
@@ -370,7 +358,7 @@ def tile_partiallyunsharedconv1d_pa_kernel(tc, x, weight, conv_bias_param, out):
                 else:
                     regroup_last(on_vector, c - 2 * LASTG, q)
                 if q + n == QUADS and c + RAWB < 2 * GROUPS:
-                    load(c + RAWB, 1)
+                    freed.append(c + RAWB)
                 u += n
 
         UNITS = (2 * GROUPS - 3) * QUADS
@@ -388,7 +376,8 @@ def tile_partiallyunsharedconv1d_pa_kernel(tc, x, weight, conv_bias_param, out):
 
         for n in range(LEAD):
             turn(n)
-        for n in range(TSTEPS + 1):
+        due = []
+        for n in range(TSTEPS + 2):
             if n + LEAD < TSTEPS:
                 turn(n + LEAD)
             if n < TSTEPS:
@@ -396,27 +385,27 @@ def tile_partiallyunsharedconv1d_pa_kernel(tc, x, weight, conv_bias_param, out):
                     evacuate(n, 0, False)
                 evacuate(n, 1, n in V_EVAC)
                 units(max(2 * n - SHIFT, 0), min(2 * n + 2 - SHIFT, UNITS))
-            if n > 0:
-                quantise(n - 1)
-                if n % QUADS == 2 and n > 2:
-                    finish(n // QUADS - 1, 0)
-                    finish(n // QUADS - 1, 1)
-            if n > 1:
-                passes(n - 2)
+            for c in due:
+                load(c, 1)
+            due = list(freed)
+            freed.clear()
+            if n % 2 == 0 and 0 < n <= TSTEPS:
+                quantise(n - 2, 2)
+            if n == TSTEPS:
+                quantise(n - 1, 1)
+            if n % QUADS == 3 and n > 3:
+                finish(n // QUADS - 1, 0)
+                finish(n // QUADS - 1, 1)
+            if n > 2:
+                passes(n - 3)
         passes(TSTEPS - 1)
         for i in range(len(PIECES_LAST) - 1):
             for a in range(QUADS):
                 regroup_last(a not in S_TAIL[i], 1, a, *PIECES_LAST[i])
-            if SPLIT_Q and i == Q_AT:
-                for a in range(QUADS):
-                    quantise_half(TSTEPS + a, 0)
         for a in range(QUADS):
             regroup_last(a not in S_TAIL[-1], 1, a, *PIECES_LAST[-1])
             for b in ([a - 1] if a > 0 else []) + ([a] if a == QUADS - 1 else []):
-                if SPLIT_Q:
-                    quantise_half(TSTEPS + b, 1)
-                else:
-                    quantise(TSTEPS + b)
+                quantise(TSTEPS + b, 1)
                 passes(TSTEPS + b)
             if a == 7:
                 finish(LASTG, 0, False)

@@ -32,12 +32,13 @@ LEAD = 2
 CH = HALF * SF
 RAWB = 4
 SHIFT = 4
+FIN_V = False
 
 KINDS = "HCC"
-S_UNITS = {"C": (1, 5, 9, 12, 16), "D": (4, 13)}
+S_UNITS = {"C": (2, 6, 11, 15), "D": ()}
 V_FIRST = (5, 6)
-PIECES_LAST = ((0, 48), (48, 16))
-S_TAIL = ((1, 2, 4, 5, 7, 8), ())
+PIECES_LAST = ((0, 64),)
+S_TAIL = ((1, 2, 4, 5, 7, 8),)
 V_EVAC = ()
 
 CUTS = ((0, 0, 15, 0), (1, 15, 29, 0), (1, 14, 15, 2), (2, 29, 44, 0), (3, 44, 64, 0), (3, 43, 44, 2))
@@ -90,7 +91,7 @@ def tile_partiallyunsharedconv1d_pa_kernel(tc, x, weight, conv_bias_param, out):
             if g == LASTG:
                 half = CO // 2
                 for o0, n in PIECES_LAST if h == 1 else ((0, half),):
-                    nc.scalar.dma_start(
+                    nc.sync.dma_start(
                         out=raw[:, o0 * PACK * SF : (o0 + n) * PACK * SF].rearrange("p (o e) -> p o e", o=n),
                         in_=wva[g][:, h * half + o0 : h * half + o0 + n, :],
                     )
@@ -341,8 +342,6 @@ def tile_partiallyunsharedconv1d_pa_kernel(tc, x, weight, conv_bias_param, out):
             if part == 1:
                 nc.sync.dma_start(out=ov[g], in_=osbs[g][:])
 
-        freed = []
-
         def units(u0, u1):
             u = u0
             while u < u1:
@@ -358,7 +357,7 @@ def tile_partiallyunsharedconv1d_pa_kernel(tc, x, weight, conv_bias_param, out):
                 else:
                     regroup_last(on_vector, c - 2 * LASTG, q)
                 if q + n == QUADS and c + RAWB < 2 * GROUPS:
-                    freed.append(c + RAWB)
+                    load(c + RAWB, 1)
                 u += n
 
         UNITS = (2 * GROUPS - 3) * QUADS
@@ -376,7 +375,6 @@ def tile_partiallyunsharedconv1d_pa_kernel(tc, x, weight, conv_bias_param, out):
 
         for n in range(LEAD):
             turn(n)
-        due = []
         for n in range(TSTEPS + 2):
             if n + LEAD < TSTEPS:
                 turn(n + LEAD)
@@ -385,29 +383,22 @@ def tile_partiallyunsharedconv1d_pa_kernel(tc, x, weight, conv_bias_param, out):
                     evacuate(n, 0, False)
                 evacuate(n, 1, n in V_EVAC)
                 units(max(2 * n - SHIFT, 0), min(2 * n + 2 - SHIFT, UNITS))
-            for c in due:
-                load(c, 1)
-            due = list(freed)
-            freed.clear()
             if n % 2 == 0 and 0 < n <= TSTEPS:
                 quantise(n - 2, 2)
             if n == TSTEPS:
                 quantise(n - 1, 1)
             if n % QUADS == 3 and n > 3:
-                finish(n // QUADS - 1, 0)
-                finish(n // QUADS - 1, 1)
+                finish(n // QUADS - 1, 0, FIN_V)
+                finish(n // QUADS - 1, 1, FIN_V)
             if n > 2:
                 passes(n - 3)
         passes(TSTEPS - 1)
-        for i in range(len(PIECES_LAST) - 1):
-            for a in range(QUADS):
-                regroup_last(a not in S_TAIL[i], 1, a, *PIECES_LAST[i])
         for a in range(QUADS):
-            regroup_last(a not in S_TAIL[-1], 1, a, *PIECES_LAST[-1])
-            for b in ([a - 1] if a > 0 else []) + ([a] if a == QUADS - 1 else []):
-                quantise(TSTEPS + b, 1)
-                passes(TSTEPS + b)
-            if a == 7:
+            regroup_last(a not in S_TAIL[0], 1, a)
+        for a in range(QUADS):
+            quantise(TSTEPS + a, 1)
+            passes(TSTEPS + a)
+            if a == 6:
                 finish(LASTG, 0, False)
                 finish(LASTG - 1, 0, False)
                 finish(LASTG - 1, 1, False)

from contextlib import ExitStack

import concourse.mybir as mybir
from concourse.masks import make_identity

FP8X4 = mybir.dt.float8_e4m3fn_x4
BF16 = mybir.dt.bfloat16
F32 = mybir.dt.float32
U32 = mybir.dt.uint32
U8 = mybir.dt.uint8
I32 = mybir.dt.int32

P = 128
GROUPS = 4
CO = 128
CI = 512
PACK = 4
L = 256
NSEG = 4
TAPS = 9
SF = NSEG * TAPS
R = 4
A = L // R
EXT = R + TAPS - 1
XCOLS = EXT * A
HALF = CI // 2
QUADS = SF // 4
PIECES = 4
STEPS = GROUPS * QUADS
TSTEPS = STEPS - QUADS
LEAD = 2
CH = HALF * SF
RAWB = 4
SHIFT = 4
FIN_V = False

KINDS = "HCC"
S_UNITS = {"C": (2, 6, 11, 15), "D": ()}
V_FIRST = (5, 6)
PIECES_LAST = ((0, 64),)
S_TAIL = ((1, 2, 4, 5, 7, 8),)
V_EVAC = ()

CUTS = ((0, 0, 15, 0), (1, 15, 29, 0), (1, 14, 15, 2), (2, 29, 44, 0), (3, 44, 64, 0), (3, 43, 44, 2))

FLOPS = 2 * GROUPS * CO * CI * TAPS * L


def tile_partiallyunsharedconv1d_pa_kernel(tc, x, weight, conv_bias_param, out):
    nc = tc.nc
    xv = x.rearrange("b d k (h p e) l -> (b d k) p h (e l)", h=2, e=2)
    xd = x.rearrange("b d k (j p) l -> (b d k) p j l", j=PACK)
    wd = weight.rearrange("d k o (j i) s u f -> (d k) (o j) (i s u f)", j=PACK)
    wh = weight.rearrange("d k o (h i) s u f -> (d k) (o h) (i s u f)", h=2)
    xva = x.rearrange("b d k (p j) l -> (b d k) p (j l)", j=PACK)
    wv = weight.rearrange("d k o i s u f -> (d k) o (i s u f)")
    wva = weight.rearrange("d k o (p j) s u f -> (d k) p o (j s u f)", j=PACK)
    bv = conv_bias_param.rearrange("d k o s u -> o (d k) (s u)")
    ov = out.rearrange("b d k o l -> (b d k) o l")
    LASTG = GROUPS - 1

    with ExitStack() as ctx:
        ctx.enter_context(tc.manual_schedule())
        keep = ctx.enter_context(tc.tile_pool(name="keep", bufs=1))
        rawp = ctx.enter_context(tc.tile_pool(name="rawp", bufs=RAWB))
        w2p = ctx.enter_context(tc.tile_pool(name="w2p", bufs=4))
        grpp = ctx.enter_context(tc.tile_pool(name="grpp", bufs=6))
        codp = ctx.enter_context(tc.tile_pool(name="codp", bufs=5))
        outp = ctx.enter_context(tc.tile_pool(name="outp", bufs=4))
        ptp = ctx.enter_context(tc.psum_pool(name="ptp", bufs=6))
        accp = ctx.enter_context(tc.psum_pool(name="accp", bufs=2))

        cold = keep.tile([P, 1], F32)
        warm = keep.tile([P, 1], F32)
        nc.vector.memset(cold[:], 0.0)
        nc.scalar.activation(out=warm[:], in_=cold[:], func=mybir.ActivationFunctionType.Identity)
        ident = keep.tile([P, P], F32)
        make_identity(nc, ident[:])
        ident_b = keep.tile([P, P], BF16)
        nc.vector.tensor_copy(out=ident_b[:], in_=ident[:])
        bias_bf = keep.tile([P, GROUPS * NSEG], BF16)
        nc.gpsimd.dma_start(out=bias_bf[:].rearrange("o (g s) -> o g s", s=NSEG), in_=bv)

        raws = {}
        w2s = {}

        def load(c, pieces):
            raw = rawp.tile([P, CH], BF16, name="raw")
            raws[c] = raw
            g, h = divmod(c, 2)
            if g == LASTG:
                half = CO // 2
                for o0, n in PIECES_LAST if h == 1 else ((0, half),):
                    nc.sync.dma_start(
                        out=raw[:, o0 * PACK * SF : (o0 + n) * PACK * SF].rearrange("p (o e) -> p o e", o=n),
                        in_=wva[g][:, h * half + o0 : h * half + o0 + n, :],
                    )
            elif KINDS[g] == "D":
                for i in range(2):
                    r0 = (2 * h + i) * P
                    nc.sync.dma_start(out=raw[:, i * CH // 2 : (i + 1) * CH // 2], in_=wd[g][r0 : r0 + P, :])
            else:
                w = CH // pieces
                for i in range(pieces):
                    if KINDS[g] == "H":
                        src = wh[g][h * P : (h + 1) * P, i * w : (i + 1) * w]
                    else:
                        src = wv[g][:, h * CH + i * w : h * CH + (i + 1) * w]
                    nc.sync.dma_start(out=raw[:, i * w : (i + 1) * w], in_=src)

        def copy(on_vector, dst, src):
            if on_vector:
                nc.vector.tensor_copy(out=dst, in_=src)
            else:
                nc.scalar.copy(out=dst, in_=src)

        def regroup(on_vector, c, q0, q1, m0, m1):
            if c not in w2s:
                w2 = w2p.tile([P, SF, HALF], BF16, name="w2", align_bytes=64)
                w2s[c] = w2
            if KINDS[c // 2] == "D":
                words = w2s[c][:].rearrange("p f m -> p (f m)").bitcast(F32).rearrange("p (m t i) -> p t i m", m=SF // 2, t=2)
                raw = raws[c][:].bitcast(F32).rearrange("p (t i m) -> p t i m", t=2, m=SF // 2)
                copy(on_vector, words[:, :, :, 2 * q0 : 2 * q1], raw[:, :, :, 2 * q0 : 2 * q1])
                return
            src = raws[c][:, m0 * SF : m1 * SF].rearrange("p (m a q) -> p a m q", a=QUADS, q=4)
            dst = w2s[c][:, :, m0:m1].rearrange("p (a q) m -> p a m q", q=4)
            copy(on_vector, dst[:, q0:q1], src[:, q0:q1])

        gas = {}
        ROWS = SF // 2

        def regroup_last(on_vector, h, a, o0=0, n_o=CO // 2):
            m0, m1 = o0 * PACK, (o0 + n_o) * PACK
            src = raws[2 * LASTG + h][:, m0 * SF : m1 * SF].rearrange("p (m a q) -> p a m q", a=QUADS, q=4)
            sf = 4 * a
            while sf < 4 * a + 4:
                t, r0 = divmod(sf, ROWS)
                n = min(4 * a + 4 - sf, ROWS - r0)
                if t not in gas:
                    ga = w2p.tile([P, ROWS, CO * PACK], BF16, name="w2", align_bytes=64)
                    gas[t] = ga
                dst = gas[t][:, r0 : r0 + n, h * HALF + m0 : h * HALF + m1].rearrange("p (a q) m -> p a m q", q=n)
                copy(on_vector, dst, src[:, a : a + 1, :, sf - 4 * a : sf - 4 * a + n])
                sf += n

        XR = 2 * PACK * L
        xts = {}

        def load_x(j):
            xt = w2p.tile([P, CH], BF16, name="w2", align_bytes=64)
            xts[j] = xt
            for i in range(2):
                g = 2 * j + i
                dst = xt[:, i * PACK * L : (i + 1) * PACK * L]
                if g == LASTG:
                    nc.sync.dma_start(out=dst, in_=xva[g])
                elif KINDS[g] == "D":
                    nc.sync.dma_start(out=dst.rearrange("p (j l) -> p j l", j=PACK), in_=xd[g])
                else:
                    nc.sync.dma_start(out=dst.rearrange("p (h w) -> p h w", h=2), in_=xv[g])

        load(0, PIECES)
        load_x(0)
        load(1, PIECES)
        load_x(1)
        for c in range(2, RAWB):
            load(c, 1)

        mp = HALF // PIECES

        def first_pieces(on_vector, c):
            q0, q1 = (0, V_FIRST[c]) if on_vector else (V_FIRST[c], QUADS)
            for i in range(PIECES):
                regroup(on_vector, c, q0, q1, i * mp, (i + 1) * mp)

        xc = keep.tile([P, GROUPS * XCOLS], U32, align_bytes=64)
        xs = keep.tile([P, GROUPS * XCOLS], U8, align_bytes=64)
        xci = xc[:].bitcast(I32).rearrange("p (g r a) -> p g r a", g=GROUPS, r=EXT)
        xsi = xs[:].rearrange("p (g r a) -> p g r a", g=GROUPS, r=EXT)
        for plane in (xci, xsi):
            nc.vector.memset(plane[:, :, 0:R, 0:1], 0)
            nc.vector.memset(plane[:, :, 2 * R : EXT, A - 1 : A], 0)

        def x_base(j, on_vector):
            for i in range(2):
                src = xts[j][:, i * PACK * L : (i + 1) * PACK * L].rearrange("p (t a r) -> p r a t", t=PACK, r=R)
                dst = xts[j][:, XR + i * PACK * L : XR + (i + 1) * PACK * L].rearrange("p (r a t) -> p r a t", r=R, t=PACK)
                copy(on_vector, dst, src)

        def x_quantise(j):
            for i in range(2):
                c0 = (2 * j + i) * XCOLS + R * A
                nc.vector.quantize_mx(
                    out=xc[:, c0 : c0 + R * A].bitcast(FP8X4),
                    scales=xs[:, c0 : c0 + R * A],
                    in_=xts[j][:, XR + i * PACK * L : XR + (i + 1) * PACK * L],
                )

        def x_shift(j):
            for plane in (xci[:, 2 * j : 2 * j + 2], xsi[:, 2 * j : 2 * j + 2]):
                nc.vector.tensor_copy(out=plane[:, :, 0:R, 1:A], in_=plane[:, :, R : 2 * R, 0 : A - 1])
                nc.vector.tensor_copy(out=plane[:, :, 2 * R : EXT, 0 : A - 1], in_=plane[:, :, R : 2 * R, 1:A])

        bias_f = keep.tile([P, GROUPS * NSEG], F32)
        first_pieces(True, 0)
        first_pieces(False, 0)
        x_base(0, True)
        x_quantise(0)
        x_shift(0)
        nc.vector.tensor_copy(out=bias_f[:], in_=bias_bf[:])
        first_pieces(True, 1)
        load(RAWB, 1)

        pts = {}
        grps = {}
        pairs = {}
        cods = {}
        accs = {}
        osbs = {}

        def transposes(n, halves=(0, 1)):
            g, a = divmod(n, QUADS)
            for b in halves:
                if KINDS[g] == "H":
                    pt = ptp.tile([P, 4, P], F32, name="pt")
                    pts[(n, b)] = pt
                    for s in range(4):
                        nc.tensor.transpose(pt[:, s, :], w2s[2 * g + b][:, 4 * a + s, :].bitcast(F32), ident[:])
                    continue
                if KINDS[g] == "D":
                    pt = ptp.tile([P, 4, 2, P], BF16, name="pt")
                    pts[(n, b)] = pt
                    src = w2s[2 * g + b][:].rearrange("p (m v) i -> p m (v i)", v=2)
                    src = src.rearrange("p m (t i w) -> p m w t i", t=2, w=2)
                    for s in range(4):
                        for t in range(2):
                            nc.tensor.transpose(pt[:, s, t, :], src[:, 2 * a + s // 2, s % 2, t, :], ident_b[:])
                    continue
                pt = ptp.tile([P, 2, 2, CO], F32, name="pt")
                pts[(n, b)] = pt
                for s in range(2):
                    sf = 4 * a + 2 * b + s
                    for h in range(2):
                        nc.tensor.transpose(pt[:, s, h, :], w2s[2 * g + h][:, sf, :].bitcast(F32), ident[:])

        W = 4 * CO * PACK

        def evacuate(n, b, on_vector):
            if n not in grps:
                grp = grpp.tile([P, 2 * W], BF16, name="grp", align_bytes=64)
                pairs[n // 2] = grp[:]
                for i in range(2):
                    grps[n - n % 2 + i] = grp[:, i * W : (i + 1) * W]
            half = CO // 2 * PACK
            if KINDS[n // QUADS] == "H":
                dst = grps[n].bitcast(F32).rearrange("p (s m) -> p s m", s=4)[:, :, b * P : (b + 1) * P]
                copy(on_vector, dst, pts[(n, b)][:])
                return
            if KINDS[n // QUADS] == "D":
                dst = grps[n].rearrange("p (s m) -> p s m", s=4)[:, :, b * half : (b + 1) * half]
                copy(on_vector, dst, pts[(n, b)][:].rearrange("p s t o -> p s (t o)"))
                return
            half = CO * PACK
            dst = grps[n].bitcast(F32)[:, b * half : (b + 1) * half].rearrange("p (s o h) -> p s o h", s=2, h=2)
            copy(on_vector, dst, pts[(n, b)][:].rearrange("p s h o -> p s o h"))

        def code_tiles(n):
            t, j = divmod(n, 2)
            if t not in cods:
                wc = codp.tile([P, 2 * 4 * CO], U32, name="wc", align_bytes=64)
                ws = codp.tile([P, 2 * 4 * CO], U8, name="ws", align_bytes=64)
                cods[t] = (wc, ws)
            return cods[t], j * 4 * CO

        def quantise(n, quads):
            (wc, ws), c0 = code_tiles(n)
            if n < TSTEPS:
                whole = grps[n] if quads == 1 else pairs[n // 2]
                parts = [whole]
            else:
                parts = []
                sf = 4 * (n - TSTEPS)
                while sf < 4 * (n - TSTEPS) + 4:
                    k, r0 = divmod(sf, ROWS)
                    m = min(4 * (n - TSTEPS) + 4 - sf, ROWS - r0)
                    parts.append(gas[k][:, r0 : r0 + m, :].rearrange("p s m -> p (s m)"))
                    sf += m
            w = quads * 4 * CO // len(parts)
            for i, part in enumerate(parts):
                nc.vector.quantize_mx(
                    out=wc[:, c0 + i * w : c0 + (i + 1) * w].bitcast(FP8X4),
                    scales=ws[:, c0 + i * w : c0 + (i + 1) * w],
                    in_=part,
                )

        def passes(n):
            g, a = divmod(n, QUADS)
            (wc, ws), base = code_tiles(n)
            for i in range(4):
                s, f = divmod(4 * a + i, TAPS)
                if f == 0 and s % 2 == 0:
                    if g == LASTG:
                        bank = ptp.tile([P, 2 * L], F32, name="pt")
                    else:
                        bank = accp.tile([P, 2 * L], F32, name="bank")
                    accs[(g, s // 2)] = bank
                acc = accs[(g, s // 2)][:, (s % 2) * L : (s % 2 + 1) * L]
                x0 = g * XCOLS + A * f
                c0 = base + i * CO
                nc.tensor.matmul_mx(
                    out=acc,
                    lhsT=wc[:, c0 : c0 + CO].bitcast(FP8X4),
                    lhsT_scale=ws[:, c0 : c0 + CO],
                    rhs=xc[:, x0 : x0 + L].bitcast(FP8X4),
                    rhs_scale=xs[:, x0 : x0 + L],
                    start=(f == 0),
                    stop=(f == TAPS - 1),
                )

        def finish(g, part, on_vector=True):
            if part == 0:
                osb = outp.tile([P, L], F32, name="osb")
                osbs[g] = osb
            oar = osbs[g][:].rearrange("p (a r) -> p a r", r=R)
            for s, a0, a1, r0 in CUTS[3 * part : 3 * part + 3]:
                acc = accs[(g, s // 2)][:, (s % 2) * L : (s % 2 + 1) * L].rearrange("p (r a) -> p a r", r=R)
                if on_vector:
                    nc.vector.tensor_scalar_add(
                        out=oar[:, a0:a1, r0:R],
                        in0=acc[:, a0:a1, r0:R],
                        scalar1=bias_f[:, g * NSEG + s : g * NSEG + s + 1],
                    )
                else:
                    nc.scalar.activation(
                        out=oar[:, a0:a1, r0:R],
                        in_=acc[:, a0:a1, r0:R],
                        func=mybir.ActivationFunctionType.Identity,
                        bias=bias_f[:, g * NSEG + s : g * NSEG + s + 1],
                        scale=1.0,
                    )
            if part == 1:
                nc.sync.dma_start(out=ov[g], in_=osbs[g][:])

        def units(u0, u1):
            u = u0
            while u < u1:
                c, q = divmod(u, QUADS)
                c += 2
                kind = KINDS[c // 2] if c < 2 * LASTG else "C"
                on_vector = (u % (2 * QUADS)) not in S_UNITS[kind]
                n = 1
                if u + 1 < u1 and q + 1 < QUADS and c < 2 * LASTG and on_vector and ((u + 1) % (2 * QUADS)) not in S_UNITS[kind]:
                    n = 2
                if c < 2 * LASTG:
                    regroup(on_vector, c, q, q + n, 0, HALF)
                else:
                    regroup_last(on_vector, c - 2 * LASTG, q)
                if q + n == QUADS and c + RAWB < 2 * GROUPS:
                    load(c + RAWB, 1)
                u += n

        UNITS = (2 * GROUPS - 3) * QUADS
        for n in range(QUADS):
            transposes(n, (0,))
            evacuate(n, 0, False)
        first_pieces(False, 1)
        load(RAWB + 1, 1)
        x_base(1, True)
        x_quantise(1)
        x_shift(1)

        def turn(n):
            transposes(n, (1,) if n < QUADS else (0, 1))

        for n in range(LEAD):
            turn(n)
        for n in range(TSTEPS + 2):
            if n + LEAD < TSTEPS:
                turn(n + LEAD)
            if n < TSTEPS:
                if n >= QUADS:
                    evacuate(n, 0, False)
                evacuate(n, 1, n in V_EVAC)
                units(max(2 * n - SHIFT, 0), min(2 * n + 2 - SHIFT, UNITS))
            if n % 2 == 0 and 0 < n <= TSTEPS:
                quantise(n - 2, 2)
            if n == TSTEPS:
                quantise(n - 1, 1)
            if n % QUADS == 3 and n > 3:
                finish(n // QUADS - 1, 0, FIN_V)
                finish(n // QUADS - 1, 1, FIN_V)
            if n > 2:
                passes(n - 3)
        passes(TSTEPS - 1)
        for a in range(QUADS):
            regroup_last(a not in S_TAIL[0], 1, a)
        for a in range(QUADS):
            quantise(TSTEPS + a, 1)
            passes(TSTEPS + a)
            if a == 6:
                finish(LASTG, 0, False)
                finish(LASTG - 1, 0, False)
                finish(LASTG - 1, 1, False)
        finish(LASTG, 1, False)
